import numpy as np
import ml_dtypes


def mxq(x, axis, fmt="e4m3"):
    dtype, down = {"e4m3": (ml_dtypes.float8_e4m3fn, 7), "e5m2": (ml_dtypes.float8_e5m2, 14)}[fmt]
    v = np.moveaxis(np.asarray(x, np.float32).astype(ml_dtypes.bfloat16).astype(np.float64), axis, -1)
    blocks = v.reshape(v.shape[:-1] + (-1, 32))
    amax = np.abs(blocks).max(-1, keepdims=True)
    byte = np.maximum(np.where(amax > 0, np.frexp(amax)[1] - 1 + 127, 0) - down, 1)
    scale = np.exp2(byte - 127.0)
    codes = (blocks / scale).astype(np.float32).astype(dtype).astype(np.float64)
    return np.moveaxis((codes * scale).reshape(v.shape), -1, axis)


WIDE = False


def mx_kscale(k):
    if not WIDE:
        return np.ones(k)
    levels = np.array([10, -10, 5, -5, 0])
    a = np.random.permutation(np.resize(levels, k // 512 * 4)).reshape(k // 512, 4)
    idx = np.arange(k)
    return np.exp2(a[idx // 512, idx % 128 // 32])


BF16 = ml_dtypes.bfloat16


def bf(x):
    return np.asarray(x, np.float32).astype(BF16)


def f64(x):
    return np.asarray(x).astype(np.float64)


E2M1 = np.array([0.0, 0.5, 1.0, 1.5, 2.0, 3.0, 4.0, 6.0, -0.0, -0.5, -1.0, -1.5, -2.0, -3.0, -4.0, -6.0])


def pack_weight(w, fmt):
    k, n = w.shape
    w = f64(bf(w)).reshape(k // 32, 32, n)
    amax = np.abs(w).max(1)
    if fmt == "e4m3":
        byte = np.frexp(amax)[1] - 1 + 127 - 7
    else:
        mant, ex = np.frexp(amax / 6.0)
        byte = np.where(mant > 0.5, ex, ex - 1) + 127
    byte = np.clip(np.where(amax > 0, byte, 1), 1, 254)
    scaled = (w * np.exp2(127.0 - byte)[:, None, :]).reshape(k, n).astype(np.float32)
    by_word = np.ascontiguousarray(scaled.reshape(k // 512, 128, 4, n).transpose(0, 1, 3, 2))
    if fmt == "e4m3":
        words = by_word.astype(ml_dtypes.float8_e4m3fn).view(np.uint8)
    else:
        c = by_word.astype(ml_dtypes.float4_e2m1fn).view(np.uint8) & 0xF
        words = c[..., 0::2] | (c[..., 1::2] << 4)
    return np.ascontiguousarray(words), np.ascontiguousarray(byte.astype(np.uint8).reshape(k // 512, 16, n))


def unpack_weight(words, scales, fmt):
    g, p, n, _ = words.shape
    if fmt == "e4m3":
        vals = np.ascontiguousarray(words).view(ml_dtypes.float8_e4m3fn).astype(np.float64)
    else:
        nib = np.empty((g, p, n, 4), np.uint8)
        nib[..., 0::2] = words & 0xF
        nib[..., 1::2] = words >> 4
        vals = E2M1[nib]
    vals = vals * np.repeat(np.exp2(scales.astype(np.float64) - 127.0), 8, axis=1)[..., None]
    return vals.transpose(0, 1, 3, 2).reshape(g * 512, n)


B, I, H = 4096, 512, 512
DT = 0.1
FMT = "e4m3"


def sigmoid(v):
    return 1.0 / (1.0 + np.exp(-v))


def setup_inputs():
    s = mx_kscale(I)
    wt = np.random.standard_normal((H, I + H)) * 1.5 / np.sqrt(I + H)
    wt[:, :I] = wt[:, :I] / s
    x = bf(np.random.standard_normal((B, I)) * s)
    hidden = bf(np.random.standard_normal((B, H)))
    W_rec_words, W_rec_scales = pack_weight((np.random.standard_normal((H, H)) * 1.0 / np.sqrt(H)).T, FMT)
    W_in_w_words, W_in_w_scales = pack_weight((np.random.standard_normal((H, I)) * 0.8 / np.sqrt(I) / s).T, FMT)
    W_in_b = bf(np.random.standard_normal(H) * 0.5)
    tau_base = bf(0.3 + 0.3 * np.random.random(H))
    tau_adapt_w_words, tau_adapt_w_scales = pack_weight(wt.T, FMT)
    tau_adapt_b = bf(np.random.standard_normal(H) * 0.5)
    return {"x": x,
            "hidden": hidden,
            "W_rec_words": W_rec_words,
            "W_rec_scales": W_rec_scales,
            "W_in_w_words": W_in_w_words,
            "W_in_w_scales": W_in_w_scales,
            "W_in_b": W_in_b,
            "tau_base": tau_base,
            "tau_adapt_w_words": tau_adapt_w_words,
            "tau_adapt_w_scales": tau_adapt_w_scales,
            "tau_adapt_b": tau_adapt_b}


def reference(x, hidden, W_rec_words, W_rec_scales, W_in_w_words, W_in_w_scales, W_in_b, tau_base, tau_adapt_w_words, tau_adapt_w_scales, tau_adapt_b):
    h = f64(hidden)
    wt_t = unpack_weight(tau_adapt_w_words, tau_adapt_w_scales, FMT)
    xq = mxq(f64(x), 1, "e4m3")
    hq = mxq(h, 1, "e4m3")
    input_contrib = (xq @ unpack_weight(W_in_w_words, W_in_w_scales, FMT)) + f64(W_in_b)
    x_tau = xq @ wt_t[:I]
    tau_logits = x_tau + (hq @ wt_t[I:]) + f64(tau_adapt_b)
    tau = f64(tau_base) * (0.5 + sigmoid(tau_logits))
    activated = np.tanh((hq @ unpack_weight(W_rec_words, W_rec_scales, FMT)) + input_contrib)
    return h + DT * (-h + activated) / tau

@@ -1,0 +1,243 @@
+import math
+from contextlib import ExitStack
+
+import concourse.mybir as mybir
+from concourse.masks import make_identity
+
+F32 = mybir.dt.float32
+BF16 = mybir.dt.bfloat16
+U8 = mybir.dt.uint8
+U32 = mybir.dt.uint32
+I32 = mybir.dt.int32
+FP8X4 = mybir.dt.float8_e4m3fn_x4
+TANH = mybir.ActivationFunctionType.Tanh
+ALU = mybir.AluOpType
+
+P = 128
+PACK = 4
+BATCH = 4096
+FEATURES = 512
+WORDS = FEATURES // 2
+ROW_TILES = BATCH // P
+CHUNK_TILES = 4
+CHUNK = CHUNK_TILES * P
+CHUNKS = ROW_TILES // CHUNK_TILES
+FEATURE_TILES = FEATURES // P
+UNITS = CHUNKS * FEATURE_TILES
+LEAD = 5
+LAG = 5
+
+W_IN = 0
+W_REC = 1
+W_TAU_X = 2
+W_TAU_H = 3
+
+FLOPS = 4 * 2 * BATCH * FEATURES * FEATURES
+
+
+def tile_liquidcell_pa_t_kernel(
+    tc,
+    x,
+    hidden,
+    W_rec_words,
+    W_rec_scales,
+    W_in_w_words,
+    W_in_w_scales,
+    W_in_b,
+    tau_base,
+    tau_adapt_w_words,
+    tau_adapt_w_scales,
+    tau_adapt_b,
+    out,
+):
+    nc = tc.nc
+
+    x_rows = x.rearrange("(p i) k -> p i k", i=ROW_TILES)
+    h_rows = hidden.rearrange("(p i) k -> p i k", i=ROW_TILES)
+    out_rows = out.rearrange("(p i) f -> p i f", i=ROW_TILES)
+
+    with ExitStack() as stack:
+        consts = stack.enter_context(tc.tile_pool(name="consts", bufs=1))
+        stage = stack.enter_context(tc.tile_pool(name="stage", bufs=2))
+        work = stack.enter_context(tc.tile_pool(name="work", bufs=3))
+        psum = stack.enter_context(tc.psum_pool(name="psum", bufs=1))
+        stack.enter_context(tc.manual_schedule())
+
+        x_nat = [consts.tile([P, CHUNK_TILES, FEATURES], BF16, name="x_nat%d" % c) for c in range(CHUNKS)]
+        h_nat = [consts.tile([P, CHUNK_TILES, FEATURES], BF16, name="h_nat%d" % c) for c in range(CHUNKS)]
+
+        def load_chunk(c):
+            tiles = slice(c * CHUNK_TILES, (c + 1) * CHUNK_TILES)
+            nc.sync.dma_start(out=x_nat[c][:], in_=x_rows[:, tiles, :])
+            nc.sync.dma_start(out=h_nat[c][:], in_=h_rows[:, tiles, :])
+
+        load_chunk(0)
+
+        vec_rows = consts.tile([P, P], BF16)
+        nc.vector.memset(vec_rows[:], 0.0)
+        for place, vec in enumerate((W_in_b, tau_adapt_b, tau_base)):
+            nc.scalar.dma_start(
+                out=vec_rows[place * FEATURE_TILES : (place + 1) * FEATURE_TILES, :],
+                in_=vec.rearrange("(j m) -> j m", m=P),
+            )
+
+        w_scales = consts.tile([P, 4, FEATURES], U8, align_bytes=64)
+        nc.vector.memset(w_scales[:].rearrange("p w n -> p (w n)").bitcast(I32), 0)
+        for quad in range(4):
+            rows = slice(4 * quad, 4 * quad + 4)
+            parts = slice(32 * quad, 32 * quad + 4)
+            nc.sync.dma_start(out=w_scales[parts, W_IN, :].bitcast(I32), in_=W_in_w_scales[0, rows, :].bitcast(I32))
+            nc.sync.dma_start(out=w_scales[parts, W_REC, :].bitcast(I32), in_=W_rec_scales[0, rows, :].bitcast(I32))
+            nc.sync.dma_start(
+                out=w_scales[parts, W_TAU_X : W_TAU_H + 1, :].bitcast(I32),
+                in_=tau_adapt_w_scales[:, rows, :].rearrange("g r n -> r g n").bitcast(I32),
+            )
+
+        w_codes = consts.tile([P, 4, FEATURES], U32, align_bytes=64)
+        nc.sync.dma_start(
+            out=w_codes[:, W_TAU_X : W_TAU_H + 1, :].bitcast(I32),
+            in_=tau_adapt_w_words.rearrange("g p n t -> p g (n t)").bitcast(I32),
+        )
+        nc.sync.dma_start(
+            out=w_codes[:, W_IN, :].bitcast(I32), in_=W_in_w_words[0].rearrange("p n t -> p (n t)").bitcast(I32)
+        )
+        nc.sync.dma_start(
+            out=w_codes[:, W_REC, :].bitcast(I32), in_=W_rec_words[0].rearrange("p n t -> p (n t)").bitcast(I32)
+        )
+
+        for c in range(1, CHUNKS):
+            load_chunk(c)
+
+        ident_f32 = consts.tile([P, P], F32)
+        make_identity(nc, ident_f32[:])
+        ident_bf16 = consts.tile([P, P], BF16)
+        make_identity(nc, ident_bf16[:])
+
+        zero_col = consts.tile([P, 1], F32)
+        nc.vector.memset(zero_col[:], 0.0)
+        warm_col = consts.tile([P, 1], F32)
+        nc.scalar.activation(out=warm_col[:], in_=zero_col[:], func=TANH)
+
+        vec_cols = psum.tile([P, P], BF16, tag="h_t", bufs=2)
+        nc.tensor.transpose(vec_cols[:], vec_rows[:], ident_bf16[:])
+        in_bias = consts.tile([P, FEATURE_TILES], F32)
+        nc.vector.tensor_copy(out=in_bias[:], in_=vec_cols[:, 0:FEATURE_TILES])
+        gate_bias = consts.tile([P, FEATURE_TILES], F32)
+        nc.vector.tensor_scalar(
+            out=gate_bias[:],
+            in0=vec_cols[:, FEATURE_TILES : 2 * FEATURE_TILES],
+            scalar1=0.5,
+            scalar2=0.5 * math.log(3.0),
+            op0=ALU.mult,
+            op1=ALU.add,
+        )
+        tau_cols = consts.tile([P, FEATURE_TILES], F32)
+        nc.vector.tensor_copy(out=tau_cols[:], in_=vec_cols[:, 2 * FEATURE_TILES : 3 * FEATURE_TILES])
+        inv_tau = consts.tile([P, FEATURE_TILES], F32)
+        nc.vector.reciprocal(out=inv_tau[:], in_=tau_cols[:])
+        neg_rate = consts.tile([P, FEATURE_TILES], F32)
+        nc.vector.tensor_scalar_mul(out=neg_rate[:], in0=inv_tau[:], scalar1=-0.2 / 3.0)
+        two_rate = consts.tile([P, FEATURE_TILES], F32)
+        nc.vector.tensor_scalar_mul(out=two_rate[:], in0=inv_tau[:], scalar1=0.4 / 3.0)
+
+        grouped = {}
+        act = {}
+
+        def transpose_pair(index):
+            chunk, part = divmod(index, 4)
+            operand, pair = divmod(part, 2)
+            natural = (x_nat, h_nat)[operand][chunk]
+            if pair == 0:
+                grouped[operand] = stage.tile([P, PACK * CHUNK], BF16, name="grouped", align_bytes=64)
+            words_t = psum.tile([P, 2, 2, P], F32, name="words_t", bufs=1)
+            for t in range(2):
+                words = natural[:, 2 * pair + t, :].bitcast(F32)
+                for u in range(2):
+                    nc.tensor.transpose(words_t[:, t, u, :], words[:, u:WORDS:2], ident_f32[:])
+            half = slice(pair * CHUNK, (pair + 1) * CHUNK)
+            nc.scalar.copy(
+                out=grouped[operand][:].bitcast(F32)[:, half].rearrange("p (t r u) -> p t r u", t=2, u=2),
+                in_=words_t[:].rearrange("p t u r -> p t r u"),
+            )
+            if pair == 1:
+                codes = stage.tile([P, CHUNK], U32, name="codes%d" % operand, align_bytes=64)
+                scales = stage.tile([P, CHUNK], U8, name="scales%d" % operand, align_bytes=64)
+                nc.vector.quantize_mx(out=codes[:].bitcast(FP8X4), scales=scales[:], in_=grouped[operand][:])
+                act[(chunk, operand)] = (codes, scales)
+
+        step_t = {}
+        pending = {}
+
+        def mx_pass(acc, weight, cols, chunk, operand, first):
+            codes, scales = act[(chunk, operand)]
+            nc.tensor.matmul_mx(
+                out=acc[:],
+                lhsT=w_codes[:, weight, cols].bitcast(FP8X4),
+                lhsT_scale=w_scales[:, weight, cols],
+                rhs=codes[:].bitcast(FP8X4),
+                rhs_scale=scales[:],
+                start=first,
+                stop=not first,
+            )
+
+        def unit_front(unit):
+            chunk, j = divmod(unit, FEATURE_TILES)
+            cols = slice(j * P, (j + 1) * P)
+            h_t = psum.tile([P, CHUNK], BF16, name="h_t", bufs=2)
+            for t in range(CHUNK_TILES):
+                nc.tensor.transpose(h_t[:, t * P : (t + 1) * P], h_nat[chunk][:, t, cols], ident_bf16[:])
+            gate_sum = psum.tile([P, CHUNK], F32, tag="sums", bufs=3)
+            mx_pass(gate_sum, W_TAU_X, cols, chunk, 0, True)
+            mx_pass(gate_sum, W_TAU_H, cols, chunk, 1, False)
+            cell_sum = psum.tile([P, CHUNK], F32, tag="sums", bufs=3)
+            mx_pass(cell_sum, W_IN, cols, chunk, 0, True)
+            mx_pass(cell_sum, W_REC, cols, chunk, 1, False)
+
+            gate = work.tile([P, CHUNK], F32)
+            nc.scalar.activation(out=gate[:], in_=gate_sum[:], func=TANH, bias=gate_bias[:, j : j + 1], scale=0.5)
+            cell = work.tile([P, CHUNK], F32)
+            nc.scalar.activation(out=cell[:], in_=cell_sum[:], func=TANH, bias=in_bias[:, j : j + 1], scale=1.0)
+            nc.vector.tensor_scalar(
+                out=gate[:],
+                in0=gate[:],
+                scalar1=neg_rate[:, j : j + 1],
+                scalar2=two_rate[:, j : j + 1],
+                op0=ALU.mult,
+                op1=ALU.add,
+            )
+            nc.vector.tensor_tensor(out=cell[:], in0=cell[:], in1=h_t[:], op=ALU.subtract)
+            pending[unit] = (gate, cell)
+
+        def unit_tail(unit):
+            chunk, j = divmod(unit, FEATURE_TILES)
+            if j == 0:
+                step_t[chunk] = work.tile([P, FEATURE_TILES, CHUNK], F32, name="step_t")
+            gate, cell = pending[unit]
+            nc.vector.tensor_tensor(out=step_t[chunk][:, j, :], in0=gate[:], in1=cell[:], op=ALU.mult)
+
+        result = {}
+
+        def finish_tile(index):
+            chunk, t = divmod(index, CHUNK_TILES)
+            if t == 0:
+                result[chunk] = work.tile([P, CHUNK_TILES, FEATURES], F32, name="result")
+            step_n = psum.tile([P, FEATURES], F32, name="step_n", bufs=2)
+            for j in range(FEATURE_TILES):
+                nc.tensor.transpose(
+                    step_n[:, j * P : (j + 1) * P], step_t[chunk][:, j, t * P : (t + 1) * P], ident_f32[:]
+                )
+            nc.vector.tensor_tensor(out=result[chunk][:, t, :], in0=step_n[:], in1=h_nat[chunk][:, t, :], op=ALU.add)
+            if t == CHUNK_TILES - 1:
+                tiles = slice(chunk * CHUNK_TILES, (chunk + 1) * CHUNK_TILES)
+                nc.sync.dma_start(out=out_rows[:, tiles, :], in_=result[chunk][:])
+
+        for step in range(UNITS + LEAD + LAG):
+            unit = step - LEAD
+            if step < UNITS:
+                transpose_pair(step)
+            if 0 <= unit < UNITS:
+                unit_front(unit)
+            if 0 <= unit - LAG < UNITS:
+                finish_tile(unit - LAG)
+            if 0 <= unit < UNITS:
+                unit_tail(unit)

@@ -166,7 +166,6 @@ def tile_liquidcell_pa_t_kernel(
                 act[(chunk, operand)] = (codes, scales)
 
         step_t = {}
-        pending = {}
 
         def mx_pass(acc, weight, cols, chunk, operand, first):
             codes, scales = act[(chunk, operand)]
@@ -180,9 +179,11 @@ def tile_liquidcell_pa_t_kernel(
                 stop=not first,
             )
 
-        def unit_front(unit):
+        def run_unit(unit):
             chunk, j = divmod(unit, FEATURE_TILES)
             cols = slice(j * P, (j + 1) * P)
+            if j == 0:
+                step_t[chunk] = work.tile([P, FEATURE_TILES, CHUNK], F32, name="step_t")
             h_t = psum.tile([P, CHUNK], BF16, name="h_t", bufs=2)
             for t in range(CHUNK_TILES):
                 nc.tensor.transpose(h_t[:, t * P : (t + 1) * P], h_nat[chunk][:, t, cols], ident_bf16[:])
@@ -206,38 +207,24 @@ def tile_liquidcell_pa_t_kernel(
                 op1=ALU.add,
             )
             nc.vector.tensor_tensor(out=cell[:], in0=cell[:], in1=h_t[:], op=ALU.subtract)
-            pending[unit] = (gate, cell)
-
-        def unit_tail(unit):
-            chunk, j = divmod(unit, FEATURE_TILES)
-            if j == 0:
-                step_t[chunk] = work.tile([P, FEATURE_TILES, CHUNK], F32, name="step_t")
-            gate, cell = pending[unit]
-            nc.vector.tensor_tensor(out=step_t[chunk][:, j, :], in0=gate[:], in1=cell[:], op=ALU.mult)
-
-        result = {}
+            nc.gpsimd.tensor_tensor(out=step_t[chunk][:, j, :], in0=gate[:], in1=cell[:], op=ALU.mult)
 
         def finish_tile(index):
             chunk, t = divmod(index, CHUNK_TILES)
-            if t == 0:
-                result[chunk] = work.tile([P, CHUNK_TILES, FEATURES], F32, name="result")
             step_n = psum.tile([P, FEATURES], F32, name="step_n", bufs=2)
             for j in range(FEATURE_TILES):
                 nc.tensor.transpose(
                     step_n[:, j * P : (j + 1) * P], step_t[chunk][:, j, t * P : (t + 1) * P], ident_f32[:]
                 )
-            nc.vector.tensor_tensor(out=result[chunk][:, t, :], in0=step_n[:], in1=h_nat[chunk][:, t, :], op=ALU.add)
-            if t == CHUNK_TILES - 1:
-                tiles = slice(chunk * CHUNK_TILES, (chunk + 1) * CHUNK_TILES)
-                nc.sync.dma_start(out=out_rows[:, tiles, :], in_=result[chunk][:])
+            result = work.tile([P, FEATURES], F32, bufs=4)
+            nc.vector.tensor_tensor(out=result[:], in0=step_n[:], in1=h_nat[chunk][:, t, :], op=ALU.add)
+            nc.sync.dma_start(out=out_rows[:, index, :], in_=result[:])
 
         for step in range(UNITS + LEAD + LAG):
             unit = step - LEAD
             if step < UNITS:
                 transpose_pair(step)
             if 0 <= unit < UNITS:
-                unit_front(unit)
+                run_unit(unit)
             if 0 <= unit - LAG < UNITS:
                 finish_tile(unit - LAG)
-            if 0 <= unit < UNITS:
-                unit_tail(unit)

@@ -11,6 +11,7 @@ U32 = mybir.dt.uint32
 I32 = mybir.dt.int32
 FP8X4 = mybir.dt.float8_e4m3fn_x4
 TANH = mybir.ActivationFunctionType.Tanh
+IDENTITY = mybir.ActivationFunctionType.Identity
 ALU = mybir.AluOpType
 
 P = 128
@@ -25,7 +26,7 @@ CHUNKS = ROW_TILES // CHUNK_TILES
 FEATURE_TILES = FEATURES // P
 UNITS = CHUNKS * FEATURE_TILES
 LEAD = 5
-LAG = 5
+LAG = 2
 
 W_IN = 0
 W_REC = 1
@@ -66,47 +67,52 @@ def tile_liquidcell_pa_t_kernel(
         x_nat = [consts.tile([P, CHUNK_TILES, FEATURES], BF16, name="x_nat%d" % c) for c in range(CHUNKS)]
         h_nat = [consts.tile([P, CHUNK_TILES, FEATURES], BF16, name="h_nat%d" % c) for c in range(CHUNKS)]
 
-        def load_chunk(c):
-            tiles = slice(c * CHUNK_TILES, (c + 1) * CHUNK_TILES)
-            nc.sync.dma_start(out=x_nat[c][:], in_=x_rows[:, tiles, :])
-            nc.sync.dma_start(out=h_nat[c][:], in_=h_rows[:, tiles, :])
-
-        load_chunk(0)
+        def load(queue, natural, rows, c):
+            queue.dma_start(out=natural[c][:], in_=rows[:, c * CHUNK_TILES : (c + 1) * CHUNK_TILES, :])
 
         vec_rows = consts.tile([P, P], BF16)
         nc.vector.memset(vec_rows[:], 0.0)
-        for place, vec in enumerate((W_in_b, tau_adapt_b, tau_base)):
-            nc.scalar.dma_start(
-                out=vec_rows[place * FEATURE_TILES : (place + 1) * FEATURE_TILES, :],
-                in_=vec.rearrange("(j m) -> j m", m=P),
-            )
-
         w_scales = consts.tile([P, 4, FEATURES], U8, align_bytes=64)
         nc.vector.memset(w_scales[:].rearrange("p w n -> p (w n)").bitcast(I32), 0)
-        for quad in range(4):
+
+        def load_scales(quad):
             rows = slice(4 * quad, 4 * quad + 4)
             parts = slice(32 * quad, 32 * quad + 4)
-            nc.sync.dma_start(out=w_scales[parts, W_IN, :].bitcast(I32), in_=W_in_w_scales[0, rows, :].bitcast(I32))
-            nc.sync.dma_start(out=w_scales[parts, W_REC, :].bitcast(I32), in_=W_rec_scales[0, rows, :].bitcast(I32))
             nc.sync.dma_start(
                 out=w_scales[parts, W_TAU_X : W_TAU_H + 1, :].bitcast(I32),
                 in_=tau_adapt_w_scales[:, rows, :].rearrange("g r n -> r g n").bitcast(I32),
             )
+            nc.sync.dma_start(out=w_scales[parts, W_IN, :].bitcast(I32), in_=W_in_w_scales[0, rows, :].bitcast(I32))
+            nc.sync.dma_start(out=w_scales[parts, W_REC, :].bitcast(I32), in_=W_rec_scales[0, rows, :].bitcast(I32))
+
+        load_scales(0)
+        load_scales(1)
+        load(nc.scalar, x_nat, x_rows, 0)
+        load(nc.scalar, h_nat, h_rows, 0)
+        load_scales(2)
+        load_scales(3)
+        load(nc.sync, x_nat, x_rows, 1)
 
         w_codes = consts.tile([P, 4, FEATURES], U32, align_bytes=64)
         nc.sync.dma_start(
             out=w_codes[:, W_TAU_X : W_TAU_H + 1, :].bitcast(I32),
             in_=tau_adapt_w_words.rearrange("g p n t -> p g (n t)").bitcast(I32),
         )
+        for place, vec in enumerate((W_in_b, tau_adapt_b, tau_base)):
+            nc.sync.dma_start(
+                out=vec_rows[place * FEATURE_TILES : (place + 1) * FEATURE_TILES, :],
+                in_=vec.rearrange("(j m) -> j m", m=P),
+            )
         nc.sync.dma_start(
             out=w_codes[:, W_IN, :].bitcast(I32), in_=W_in_w_words[0].rearrange("p n t -> p (n t)").bitcast(I32)
         )
         nc.sync.dma_start(
             out=w_codes[:, W_REC, :].bitcast(I32), in_=W_rec_words[0].rearrange("p n t -> p (n t)").bitcast(I32)
         )
-
-        for c in range(1, CHUNKS):
-            load_chunk(c)
+        load(nc.sync, h_nat, h_rows, 1)
+        for c in range(2, CHUNKS):
+            load(nc.sync, x_nat, x_rows, c)
+            load(nc.sync, h_nat, h_rows, c)
 
         ident_f32 = consts.tile([P, P], F32)
         make_identity(nc, ident_f32[:])
@@ -118,27 +124,29 @@ def tile_liquidcell_pa_t_kernel(
         warm_col = consts.tile([P, 1], F32)
         nc.scalar.activation(out=warm_col[:], in_=zero_col[:], func=TANH)
 
-        vec_cols = psum.tile([P, P], BF16, tag="h_t", bufs=2)
-        nc.tensor.transpose(vec_cols[:], vec_rows[:], ident_bf16[:])
         in_bias = consts.tile([P, FEATURE_TILES], F32)
-        nc.vector.tensor_copy(out=in_bias[:], in_=vec_cols[:, 0:FEATURE_TILES])
         gate_bias = consts.tile([P, FEATURE_TILES], F32)
-        nc.vector.tensor_scalar(
-            out=gate_bias[:],
-            in0=vec_cols[:, FEATURE_TILES : 2 * FEATURE_TILES],
-            scalar1=0.5,
-            scalar2=0.5 * math.log(3.0),
-            op0=ALU.mult,
-            op1=ALU.add,
-        )
         tau_cols = consts.tile([P, FEATURE_TILES], F32)
-        nc.vector.tensor_copy(out=tau_cols[:], in_=vec_cols[:, 2 * FEATURE_TILES : 3 * FEATURE_TILES])
         inv_tau = consts.tile([P, FEATURE_TILES], F32)
-        nc.vector.reciprocal(out=inv_tau[:], in_=tau_cols[:])
         neg_rate = consts.tile([P, FEATURE_TILES], F32)
-        nc.vector.tensor_scalar_mul(out=neg_rate[:], in0=inv_tau[:], scalar1=-0.2 / 3.0)
         two_rate = consts.tile([P, FEATURE_TILES], F32)
-        nc.vector.tensor_scalar_mul(out=two_rate[:], in0=inv_tau[:], scalar1=0.4 / 3.0)
+
+        def spread_vectors():
+            vec_cols = psum.tile([P, P], BF16, tag="h_t", bufs=2)
+            nc.tensor.transpose(vec_cols[:], vec_rows[:], ident_bf16[:])
+            nc.vector.tensor_copy(out=in_bias[:], in_=vec_cols[:, 0:FEATURE_TILES])
+            nc.vector.tensor_scalar(
+                out=gate_bias[:],
+                in0=vec_cols[:, FEATURE_TILES : 2 * FEATURE_TILES],
+                scalar1=0.5,
+                scalar2=0.5 * math.log(3.0),
+                op0=ALU.mult,
+                op1=ALU.add,
+            )
+            nc.vector.tensor_copy(out=tau_cols[:], in_=vec_cols[:, 2 * FEATURE_TILES : 3 * FEATURE_TILES])
+            nc.vector.reciprocal(out=inv_tau[:], in_=tau_cols[:])
+            nc.vector.tensor_scalar_mul(out=neg_rate[:], in0=inv_tau[:], scalar1=-0.2 / 3.0)
+            nc.vector.tensor_scalar_mul(out=two_rate[:], in0=inv_tau[:], scalar1=0.4 / 3.0)
 
         grouped = {}
         act = {}
@@ -149,7 +157,7 @@ def tile_liquidcell_pa_t_kernel(
             natural = (x_nat, h_nat)[operand][chunk]
             if pair == 0:
                 grouped[operand] = stage.tile([P, PACK * CHUNK], BF16, name="grouped", align_bytes=64)
-            words_t = psum.tile([P, 2, 2, P], F32, name="words_t", bufs=1)
+            words_t = psum.tile([P, 2, 2, P], F32, name="words_t", bufs=2)
             for t in range(2):
                 words = natural[:, 2 * pair + t, :].bitcast(F32)
                 for u in range(2):
@@ -165,6 +173,7 @@ def tile_liquidcell_pa_t_kernel(
                 nc.vector.quantize_mx(out=codes[:].bitcast(FP8X4), scales=scales[:], in_=grouped[operand][:])
                 act[(chunk, operand)] = (codes, scales)
 
+        factors = {}
         step_t = {}
 
         def mx_pass(acc, weight, cols, chunk, operand, first):
@@ -182,15 +191,13 @@ def tile_liquidcell_pa_t_kernel(
         def run_unit(unit):
             chunk, j = divmod(unit, FEATURE_TILES)
             cols = slice(j * P, (j + 1) * P)
-            if j == 0:
-                step_t[chunk] = work.tile([P, FEATURE_TILES, CHUNK], F32, name="step_t")
             h_t = psum.tile([P, CHUNK], BF16, name="h_t", bufs=2)
             for t in range(CHUNK_TILES):
                 nc.tensor.transpose(h_t[:, t * P : (t + 1) * P], h_nat[chunk][:, t, cols], ident_bf16[:])
-            gate_sum = psum.tile([P, CHUNK], F32, tag="sums", bufs=3)
+            gate_sum = psum.tile([P, CHUNK], F32, tag="sums", bufs=2)
             mx_pass(gate_sum, W_TAU_X, cols, chunk, 0, True)
             mx_pass(gate_sum, W_TAU_H, cols, chunk, 1, False)
-            cell_sum = psum.tile([P, CHUNK], F32, tag="sums", bufs=3)
+            cell_sum = psum.tile([P, CHUNK], F32, tag="sums", bufs=2)
             mx_pass(cell_sum, W_IN, cols, chunk, 0, True)
             mx_pass(cell_sum, W_REC, cols, chunk, 1, False)
 
@@ -198,33 +205,46 @@ def tile_liquidcell_pa_t_kernel(
             nc.scalar.activation(out=gate[:], in_=gate_sum[:], func=TANH, bias=gate_bias[:, j : j + 1], scale=0.5)
             cell = work.tile([P, CHUNK], F32)
             nc.scalar.activation(out=cell[:], in_=cell_sum[:], func=TANH, bias=in_bias[:, j : j + 1], scale=1.0)
-            nc.vector.tensor_scalar(
-                out=gate[:],
-                in0=gate[:],
-                scalar1=neg_rate[:, j : j + 1],
-                scalar2=two_rate[:, j : j + 1],
-                op0=ALU.mult,
-                op1=ALU.add,
-            )
-            nc.vector.tensor_tensor(out=cell[:], in0=cell[:], in1=h_t[:], op=ALU.subtract)
-            nc.gpsimd.tensor_tensor(out=step_t[chunk][:, j, :], in0=gate[:], in1=cell[:], op=ALU.mult)
-
-        def finish_tile(index):
-            chunk, t = divmod(index, CHUNK_TILES)
-            step_n = psum.tile([P, FEATURES], F32, name="step_n", bufs=2)
-            for j in range(FEATURE_TILES):
-                nc.tensor.transpose(
-                    step_n[:, j * P : (j + 1) * P], step_t[chunk][:, j, t * P : (t + 1) * P], ident_f32[:]
+            if unit % 2 == 0:
+                nc.vector.tensor_scalar(
+                    out=gate[:],
+                    in0=gate[:],
+                    scalar1=neg_rate[:, j : j + 1],
+                    scalar2=two_rate[:, j : j + 1],
+                    op0=ALU.mult,
+                    op1=ALU.add,
                 )
-            result = work.tile([P, FEATURES], F32, bufs=4)
-            nc.vector.tensor_tensor(out=result[:], in0=step_n[:], in1=h_nat[chunk][:, t, :], op=ALU.add)
-            nc.sync.dma_start(out=out_rows[:, index, :], in_=result[:])
+            else:
+                nc.scalar.activation(
+                    out=gate[:], in_=gate[:], func=IDENTITY, bias=two_rate[:, j : j + 1], scale=neg_rate[:, j : j + 1]
+                )
+            nc.vector.tensor_tensor(out=cell[:], in0=cell[:], in1=h_t[:], op=ALU.subtract)
+            factors[unit] = (gate, cell)
+
+        def multiply_unit(unit):
+            gate, cell = factors[unit]
+            step_t[unit] = work.tile([P, CHUNK], F32, name="step_t")
+            nc.vector.tensor_tensor(out=step_t[unit][:], in0=gate[:], in1=cell[:], op=ALU.mult)
+
+        def finish_unit(unit):
+            chunk, j = divmod(unit, FEATURE_TILES)
+            cols = slice(j * P, (j + 1) * P)
+            step_n = psum.tile([P, CHUNK_TILES, P], F32, name="step_n", bufs=2)
+            for t in range(CHUNK_TILES):
+                nc.tensor.transpose(step_n[:, t, :], step_t[unit][:, t * P : (t + 1) * P], ident_f32[:])
+            result = work.tile([P, CHUNK_TILES, P], F32, bufs=4)
+            nc.vector.tensor_tensor(out=result[:], in0=step_n[:], in1=h_nat[chunk][:, :, cols], op=ALU.add)
+            nc.sync.dma_start(out=out_rows[:, chunk * CHUNK_TILES : (chunk + 1) * CHUNK_TILES, cols], in_=result[:])
 
         for step in range(UNITS + LEAD + LAG):
             unit = step - LEAD
             if step < UNITS:
                 transpose_pair(step)
+            if unit == 0:
+                spread_vectors()
             if 0 <= unit < UNITS:
                 run_unit(unit)
             if 0 <= unit - LAG < UNITS:
-                finish_tile(unit - LAG)
+                finish_unit(unit - LAG)
+            if 0 <= unit < UNITS:
+                multiply_unit(unit)

@@ -26,12 +26,12 @@ CHUNKS = ROW_TILES // CHUNK_TILES
 FEATURE_TILES = FEATURES // P
 UNITS = CHUNKS * FEATURE_TILES
 LEAD = 5
-LAG = 2
+LAG = 5
 
-W_IN = 0
-W_REC = 1
-W_TAU_X = 2
-W_TAU_H = 3
+W_TAU_X = 0
+W_TAU_H = 1
+W_IN = 2
+W_REC = 3
 
 FLOPS = 4 * 2 * BATCH * FEATURES * FEATURES
 
@@ -70,20 +70,19 @@ def tile_liquidcell_pa_t_kernel(
         def load(queue, natural, rows, c):
             queue.dma_start(out=natural[c][:], in_=rows[:, c * CHUNK_TILES : (c + 1) * CHUNK_TILES, :])
 
-        vec_rows = consts.tile([P, P], BF16)
-        nc.vector.memset(vec_rows[:], 0.0)
-        w_scales = consts.tile([P, 4, FEATURES], U8, align_bytes=64)
-        nc.vector.memset(w_scales[:].rearrange("p w n -> p (w n)").bitcast(I32), 0)
+        raw_scales = consts.tile([P, FEATURES], U8, align_bytes=64)
+        nc.vector.memset(raw_scales[:].bitcast(I32), 0)
 
         def load_scales(quad):
             rows = slice(4 * quad, 4 * quad + 4)
-            parts = slice(32 * quad, 32 * quad + 4)
-            nc.sync.dma_start(
-                out=w_scales[parts, W_TAU_X : W_TAU_H + 1, :].bitcast(I32),
-                in_=tau_adapt_w_scales[:, rows, :].rearrange("g r n -> r g n").bitcast(I32),
-            )
-            nc.sync.dma_start(out=w_scales[parts, W_IN, :].bitcast(I32), in_=W_in_w_scales[0, rows, :].bitcast(I32))
-            nc.sync.dma_start(out=w_scales[parts, W_REC, :].bitcast(I32), in_=W_rec_scales[0, rows, :].bitcast(I32))
+            for place, plane in (
+                (W_TAU_X, tau_adapt_w_scales[0]),
+                (W_TAU_H, tau_adapt_w_scales[1]),
+                (W_IN, W_in_w_scales[0]),
+                (W_REC, W_rec_scales[0]),
+            ):
+                base = 32 * quad + 4 * place
+                nc.sync.dma_start(out=raw_scales[base : base + 4, :].bitcast(I32), in_=plane[rows, :].bitcast(I32))
 
         load_scales(0)
         load_scales(1)
@@ -91,60 +90,64 @@ def tile_liquidcell_pa_t_kernel(
         load(nc.scalar, h_nat, h_rows, 0)
         load_scales(2)
         load_scales(3)
-        load(nc.sync, x_nat, x_rows, 1)
 
-        w_codes = consts.tile([P, 4, FEATURES], U32, align_bytes=64)
+        raw_codes = consts.tile([P, 4, FEATURES], I32, align_bytes=64)
         nc.sync.dma_start(
-            out=w_codes[:, W_TAU_X : W_TAU_H + 1, :].bitcast(I32),
+            out=raw_codes[:, W_TAU_X : W_TAU_H + 1, :],
             in_=tau_adapt_w_words.rearrange("g p n t -> p g (n t)").bitcast(I32),
         )
+        nc.sync.dma_start(out=raw_codes[:, W_IN, :], in_=W_in_w_words[0].rearrange("p n t -> p (n t)").bitcast(I32))
+        nc.sync.dma_start(out=raw_codes[:, W_REC, :], in_=W_rec_words[0].rearrange("p n t -> p (n t)").bitcast(I32))
+
+        vectors = []
         for place, vec in enumerate((W_in_b, tau_adapt_b, tau_base)):
-            nc.sync.dma_start(
-                out=vec_rows[place * FEATURE_TILES : (place + 1) * FEATURE_TILES, :],
-                in_=vec.rearrange("(j m) -> j m", m=P),
-            )
-        nc.sync.dma_start(
-            out=w_codes[:, W_IN, :].bitcast(I32), in_=W_in_w_words[0].rearrange("p n t -> p (n t)").bitcast(I32)
-        )
-        nc.sync.dma_start(
-            out=w_codes[:, W_REC, :].bitcast(I32), in_=W_rec_words[0].rearrange("p n t -> p (n t)").bitcast(I32)
-        )
-        load(nc.sync, h_nat, h_rows, 1)
-        for c in range(2, CHUNKS):
+            vector = consts.tile([P, FEATURE_TILES], BF16, name="vector%d" % place)
+            nc.sync.dma_start(out=vector[:], in_=vec.rearrange("(p j) -> p j", j=FEATURE_TILES))
+            vectors.append(vector)
+        for c in range(1, CHUNKS):
             load(nc.sync, x_nat, x_rows, c)
             load(nc.sync, h_nat, h_rows, c)
 
         ident_f32 = consts.tile([P, P], F32)
         make_identity(nc, ident_f32[:])
-        ident_bf16 = consts.tile([P, P], BF16)
-        make_identity(nc, ident_bf16[:])
 
         zero_col = consts.tile([P, 1], F32)
         nc.vector.memset(zero_col[:], 0.0)
         warm_col = consts.tile([P, 1], F32)
         nc.scalar.activation(out=warm_col[:], in_=zero_col[:], func=TANH)
 
+        w_scales = consts.tile([P, FEATURES], U8, align_bytes=64)
+        w_codes = consts.tile([P, 4, FEATURES], I32, align_bytes=64)
+
+        def arrange_codes(place):
+            nc.vector.tensor_copy(
+                out=w_codes[:, place, :].rearrange("p (j m) -> p j m", j=FEATURE_TILES),
+                in_=raw_codes[:, place, :].rearrange("p (m j) -> p j m", j=FEATURE_TILES),
+            )
+
+        def arrange_scales():
+            nc.vector.tensor_copy(
+                out=w_scales[:].rearrange("p (j m) -> p j m", j=FEATURE_TILES),
+                in_=raw_scales[:].rearrange("p (m j) -> p j m", j=FEATURE_TILES),
+            )
+
         in_bias = consts.tile([P, FEATURE_TILES], F32)
         gate_bias = consts.tile([P, FEATURE_TILES], F32)
-        tau_cols = consts.tile([P, FEATURE_TILES], F32)
         inv_tau = consts.tile([P, FEATURE_TILES], F32)
         neg_rate = consts.tile([P, FEATURE_TILES], F32)
         two_rate = consts.tile([P, FEATURE_TILES], F32)
 
-        def spread_vectors():
-            vec_cols = psum.tile([P, P], BF16, tag="h_t", bufs=2)
-            nc.tensor.transpose(vec_cols[:], vec_rows[:], ident_bf16[:])
-            nc.vector.tensor_copy(out=in_bias[:], in_=vec_cols[:, 0:FEATURE_TILES])
+        def prepare_vectors():
             nc.vector.tensor_scalar(
                 out=gate_bias[:],
-                in0=vec_cols[:, FEATURE_TILES : 2 * FEATURE_TILES],
+                in0=vectors[1][:],
                 scalar1=0.5,
                 scalar2=0.5 * math.log(3.0),
                 op0=ALU.mult,
                 op1=ALU.add,
             )
-            nc.vector.tensor_copy(out=tau_cols[:], in_=vec_cols[:, 2 * FEATURE_TILES : 3 * FEATURE_TILES])
-            nc.vector.reciprocal(out=inv_tau[:], in_=tau_cols[:])
+            nc.vector.tensor_copy(out=in_bias[:], in_=vectors[0][:])
+            nc.vector.reciprocal(out=inv_tau[:], in_=vectors[2][:])
             nc.vector.tensor_scalar_mul(out=neg_rate[:], in0=inv_tau[:], scalar1=-0.2 / 3.0)
             nc.vector.tensor_scalar_mul(out=two_rate[:], in0=inv_tau[:], scalar1=0.4 / 3.0)
 
@@ -156,7 +159,10 @@ def tile_liquidcell_pa_t_kernel(
             operand, pair = divmod(part, 2)
             natural = (x_nat, h_nat)[operand][chunk]
             if pair == 0:
-                grouped[operand] = stage.tile([P, PACK * CHUNK], BF16, name="grouped", align_bytes=64)
+                grouped[(chunk, operand)] = stage.tile(
+                    [P, PACK * CHUNK], BF16, name="grouped%d" % operand, bufs=2 + operand, align_bytes=64
+                )
+            packed = grouped[(chunk, operand)]
             words_t = psum.tile([P, 2, 2, P], F32, name="words_t", bufs=2)
             for t in range(2):
                 words = natural[:, 2 * pair + t, :].bitcast(F32)
@@ -164,13 +170,13 @@ def tile_liquidcell_pa_t_kernel(
                     nc.tensor.transpose(words_t[:, t, u, :], words[:, u:WORDS:2], ident_f32[:])
             half = slice(pair * CHUNK, (pair + 1) * CHUNK)
             nc.scalar.copy(
-                out=grouped[operand][:].bitcast(F32)[:, half].rearrange("p (t r u) -> p t r u", t=2, u=2),
+                out=packed[:].bitcast(F32)[:, half].rearrange("p (t r u) -> p t r u", t=2, u=2),
                 in_=words_t[:].rearrange("p t u r -> p t r u"),
             )
             if pair == 1:
                 codes = stage.tile([P, CHUNK], U32, name="codes%d" % operand, align_bytes=64)
                 scales = stage.tile([P, CHUNK], U8, name="scales%d" % operand, align_bytes=64)
-                nc.vector.quantize_mx(out=codes[:].bitcast(FP8X4), scales=scales[:], in_=grouped[operand][:])
+                nc.vector.quantize_mx(out=codes[:].bitcast(FP8X4), scales=scales[:], in_=packed[:])
                 act[(chunk, operand)] = (codes, scales)
 
         factors = {}
@@ -181,7 +187,7 @@ def tile_liquidcell_pa_t_kernel(
             nc.tensor.matmul_mx(
                 out=acc[:],
                 lhsT=w_codes[:, weight, cols].bitcast(FP8X4),
-                lhsT_scale=w_scales[:, weight, cols],
+                lhsT_scale=w_scales[4 * weight : P, cols],
                 rhs=codes[:].bitcast(FP8X4),
                 rhs_scale=scales[:],
                 start=first,
@@ -191,13 +197,10 @@ def tile_liquidcell_pa_t_kernel(
         def run_unit(unit):
             chunk, j = divmod(unit, FEATURE_TILES)
             cols = slice(j * P, (j + 1) * P)
-            h_t = psum.tile([P, CHUNK], BF16, name="h_t", bufs=2)
-            for t in range(CHUNK_TILES):
-                nc.tensor.transpose(h_t[:, t * P : (t + 1) * P], h_nat[chunk][:, t, cols], ident_bf16[:])
-            gate_sum = psum.tile([P, CHUNK], F32, tag="sums", bufs=2)
+            gate_sum = psum.tile([P, CHUNK], F32, tag="sums", bufs=4)
             mx_pass(gate_sum, W_TAU_X, cols, chunk, 0, True)
             mx_pass(gate_sum, W_TAU_H, cols, chunk, 1, False)
-            cell_sum = psum.tile([P, CHUNK], F32, tag="sums", bufs=2)
+            cell_sum = psum.tile([P, CHUNK], F32, tag="sums", bufs=4)
             mx_pass(cell_sum, W_IN, cols, chunk, 0, True)
             mx_pass(cell_sum, W_REC, cols, chunk, 1, False)
 
@@ -218,33 +221,46 @@ def tile_liquidcell_pa_t_kernel(
                 nc.scalar.activation(
                     out=gate[:], in_=gate[:], func=IDENTITY, bias=two_rate[:, j : j + 1], scale=neg_rate[:, j : j + 1]
                 )
-            nc.vector.tensor_tensor(out=cell[:], in0=cell[:], in1=h_t[:], op=ALU.subtract)
+            h_t = grouped[(chunk, 1)][:].rearrange("p (n j) -> p j n", j=PACK)[:, j, :]
+            nc.vector.tensor_tensor(out=cell[:], in0=cell[:], in1=h_t, op=ALU.subtract)
             factors[unit] = (gate, cell)
 
         def multiply_unit(unit):
-            gate, cell = factors[unit]
-            step_t[unit] = work.tile([P, CHUNK], F32, name="step_t")
-            nc.vector.tensor_tensor(out=step_t[unit][:], in0=gate[:], in1=cell[:], op=ALU.mult)
-
-        def finish_unit(unit):
             chunk, j = divmod(unit, FEATURE_TILES)
-            cols = slice(j * P, (j + 1) * P)
-            step_n = psum.tile([P, CHUNK_TILES, P], F32, name="step_n", bufs=2)
-            for t in range(CHUNK_TILES):
-                nc.tensor.transpose(step_n[:, t, :], step_t[unit][:, t * P : (t + 1) * P], ident_f32[:])
-            result = work.tile([P, CHUNK_TILES, P], F32, bufs=4)
-            nc.vector.tensor_tensor(out=result[:], in0=step_n[:], in1=h_nat[chunk][:, :, cols], op=ALU.add)
-            nc.sync.dma_start(out=out_rows[:, chunk * CHUNK_TILES : (chunk + 1) * CHUNK_TILES, cols], in_=result[:])
+            gate, cell = factors[unit]
+            if j == 0:
+                step_t[chunk] = work.tile([P, FEATURE_TILES, CHUNK], F32, name="step_t")
+            nc.vector.tensor_tensor(out=step_t[chunk][:, j, :], in0=gate[:], in1=cell[:], op=ALU.mult)
+
+        def finish_rows(row_tile):
+            chunk, t = divmod(row_tile, CHUNK_TILES)
+            step_n = psum.tile([P, FEATURE_TILES, P], F32, name="step_n", bufs=2)
+            for j in range(FEATURE_TILES):
+                nc.tensor.transpose(step_n[:, j, :], step_t[chunk][:, j, t * P : (t + 1) * P], ident_f32[:])
+            result = work.tile([P, FEATURES], F32, bufs=4)
+            nc.vector.tensor_tensor(
+                out=result[:].rearrange("p (m j) -> p m j", j=FEATURE_TILES),
+                in0=step_n[:].rearrange("p j m -> p m j"),
+                in1=h_nat[chunk][:, t, :].rearrange("p (m j) -> p m j", j=FEATURE_TILES),
+                op=ALU.add,
+            )
+            nc.sync.dma_start(out=out_rows[:, row_tile, :], in_=result[:])
 
         for step in range(UNITS + LEAD + LAG):
             unit = step - LEAD
             if step < UNITS:
                 transpose_pair(step)
-            if unit == 0:
-                spread_vectors()
+            if unit == -2:
+                arrange_scales()
+                arrange_codes(W_TAU_X)
+                arrange_codes(W_TAU_H)
+                prepare_vectors()
+            if unit == -1:
+                arrange_codes(W_IN)
+                arrange_codes(W_REC)
             if 0 <= unit < UNITS:
                 run_unit(unit)
-            if 0 <= unit - LAG < UNITS:
-                finish_unit(unit - LAG)
+            if 0 <= unit - LAG < ROW_TILES:
+                finish_rows(unit - LAG)
             if 0 <= unit < UNITS:
                 multiply_unit(unit)

@@ -20,13 +20,11 @@ BATCH = 4096
 FEATURES = 512
 WORDS = FEATURES // 2
 ROW_TILES = BATCH // P
-CHUNK_TILES = 4
-CHUNK = CHUNK_TILES * P
-CHUNKS = ROW_TILES // CHUNK_TILES
+SIZES = (2, 4, 4, 4, 4, 4, 4, 4, 2)
+STARTS = tuple(sum(SIZES[:c]) for c in range(len(SIZES)))
+CHUNKS = len(SIZES)
+WIDEST = max(SIZES) * P
 FEATURE_TILES = FEATURES // P
-UNITS = CHUNKS * FEATURE_TILES
-LEAD = 5
-LAG = 5
 
 W_TAU_X = 0
 W_TAU_H = 1
@@ -64,72 +62,76 @@ def tile_liquidcell_pa_t_kernel(
         psum = stack.enter_context(tc.psum_pool(name="psum", bufs=1))
         stack.enter_context(tc.manual_schedule())
 
-        x_nat = [consts.tile([P, CHUNK_TILES, FEATURES], BF16, name="x_nat%d" % c) for c in range(CHUNKS)]
-        h_nat = [consts.tile([P, CHUNK_TILES, FEATURES], BF16, name="h_nat%d" % c) for c in range(CHUNKS)]
+        x_nat = [consts.tile([P, SIZES[c], FEATURES], BF16, name="x_nat%d" % c) for c in range(CHUNKS)]
+        h_nat = [consts.tile([P, SIZES[c], FEATURES], BF16, name="h_nat%d" % c) for c in range(CHUNKS)]
 
-        def load(queue, natural, rows, c):
-            queue.dma_start(out=natural[c][:], in_=rows[:, c * CHUNK_TILES : (c + 1) * CHUNK_TILES, :])
+        def load(natural, rows, c):
+            nc.sync.dma_start(out=natural[c][:], in_=rows[:, STARTS[c] : STARTS[c] + SIZES[c], :])
 
-        raw_scales = consts.tile([P, FEATURES], U8, align_bytes=64)
-        nc.vector.memset(raw_scales[:].bitcast(I32), 0)
+        load(x_nat, x_rows, 0)
+        load(h_nat, h_rows, 0)
 
-        def load_scales(quad):
-            rows = slice(4 * quad, 4 * quad + 4)
-            for place, plane in (
-                (W_TAU_X, tau_adapt_w_scales[0]),
-                (W_TAU_H, tau_adapt_w_scales[1]),
-                (W_IN, W_in_w_scales[0]),
-                (W_REC, W_rec_scales[0]),
-            ):
-                base = 32 * quad + 4 * place
-                nc.sync.dma_start(out=raw_scales[base : base + 4, :].bitcast(I32), in_=plane[rows, :].bitcast(I32))
-
-        load_scales(0)
-        load_scales(1)
-        load(nc.scalar, x_nat, x_rows, 0)
-        load(nc.scalar, h_nat, h_rows, 0)
-        load_scales(2)
-        load_scales(3)
+        tau_scales_raw = consts.tile([P, 2, FEATURES], U8, align_bytes=64)
+        nc.vector.memset(tau_scales_raw[:].rearrange("p w n -> p (w n)").bitcast(I32), 0)
+        cell_scales_raw = consts.tile([P, 2, FEATURES], U8, align_bytes=64)
+        nc.vector.memset(cell_scales_raw[:].rearrange("p w n -> p (w n)").bitcast(I32), 0)
+        quads = [(slice(4 * q, 4 * q + 4), slice(32 * q, 32 * q + 4)) for q in range(4)]
+        for rows, parts in quads:
+            nc.sync.dma_start(
+                out=tau_scales_raw[parts, :, :].bitcast(I32),
+                in_=tau_adapt_w_scales[:, rows, :].rearrange("g r n -> r g n").bitcast(I32),
+            )
 
         raw_codes = consts.tile([P, 4, FEATURES], I32, align_bytes=64)
         nc.sync.dma_start(
             out=raw_codes[:, W_TAU_X : W_TAU_H + 1, :],
             in_=tau_adapt_w_words.rearrange("g p n t -> p g (n t)").bitcast(I32),
         )
+        for rows, parts in quads:
+            lower = slice(parts.start + 4, parts.stop + 4)
+            nc.sync.dma_start(out=cell_scales_raw[lower, 0, :].bitcast(I32), in_=W_in_w_scales[0, rows, :].bitcast(I32))
+            nc.sync.dma_start(out=cell_scales_raw[lower, 1, :].bitcast(I32), in_=W_rec_scales[0, rows, :].bitcast(I32))
         nc.sync.dma_start(out=raw_codes[:, W_IN, :], in_=W_in_w_words[0].rearrange("p n t -> p (n t)").bitcast(I32))
         nc.sync.dma_start(out=raw_codes[:, W_REC, :], in_=W_rec_words[0].rearrange("p n t -> p (n t)").bitcast(I32))
-
-        vectors = []
-        for place, vec in enumerate((W_in_b, tau_adapt_b, tau_base)):
-            vector = consts.tile([P, FEATURE_TILES], BF16, name="vector%d" % place)
-            nc.sync.dma_start(out=vector[:], in_=vec.rearrange("(p j) -> p j", j=FEATURE_TILES))
-            vectors.append(vector)
         for c in range(1, CHUNKS):
-            load(nc.sync, x_nat, x_rows, c)
-            load(nc.sync, h_nat, h_rows, c)
+            load(x_nat, x_rows, c)
+            load(h_nat, h_rows, c)
 
         ident_f32 = consts.tile([P, P], F32)
         make_identity(nc, ident_f32[:])
+
+        ident_bf16 = consts.tile([P, P], BF16)
+        make_identity(nc, ident_bf16[:])
+
+        vectors = []
+        for place, vec in enumerate((tau_adapt_b, W_in_b, tau_base)):
+            vector = consts.tile([P, FEATURE_TILES], BF16, name="vector%d" % place)
+            nc.gpsimd.dma_start(out=vector[:], in_=vec.rearrange("(p j) -> p j", j=FEATURE_TILES))
+            vectors.append(vector)
 
         zero_col = consts.tile([P, 1], F32)
         nc.vector.memset(zero_col[:], 0.0)
         warm_col = consts.tile([P, 1], F32)
         nc.scalar.activation(out=warm_col[:], in_=zero_col[:], func=TANH)
 
-        w_scales = consts.tile([P, FEATURES], U8, align_bytes=64)
+        tau_scales = consts.tile([P, 2, FEATURES], U8, align_bytes=64)
+        cell_scales = consts.tile([P, 2, FEATURES], U8, align_bytes=64)
         w_codes = consts.tile([P, 4, FEATURES], I32, align_bytes=64)
 
-        def arrange_codes(place):
+        def arrange(out, in_, half):
+            tiles = slice(2 * half, 2 * half + 2)
             nc.vector.tensor_copy(
-                out=w_codes[:, place, :].rearrange("p (j m) -> p j m", j=FEATURE_TILES),
-                in_=raw_codes[:, place, :].rearrange("p (m j) -> p j m", j=FEATURE_TILES),
+                out=out.rearrange("p w (j m) -> p w j m", j=FEATURE_TILES)[:, :, tiles, :],
+                in_=in_.rearrange("p w (m j) -> p w j m", j=FEATURE_TILES)[:, :, tiles, :],
             )
 
-        def arrange_scales():
-            nc.vector.tensor_copy(
-                out=w_scales[:].rearrange("p (j m) -> p j m", j=FEATURE_TILES),
-                in_=raw_scales[:].rearrange("p (m j) -> p j m", j=FEATURE_TILES),
-            )
+        def arrange_gate(half):
+            arrange(tau_scales[:], tau_scales_raw[:], half)
+            arrange(w_codes[:, W_TAU_X:W_IN, :], raw_codes[:, W_TAU_X:W_IN, :], half)
+
+        def arrange_cell(half):
+            arrange(cell_scales[:], cell_scales_raw[:], half)
+            arrange(w_codes[:, W_IN : W_REC + 1, :], raw_codes[:, W_IN : W_REC + 1, :], half)
 
         in_bias = consts.tile([P, FEATURE_TILES], F32)
         gate_bias = consts.tile([P, FEATURE_TILES], F32)
@@ -137,16 +139,20 @@ def tile_liquidcell_pa_t_kernel(
         neg_rate = consts.tile([P, FEATURE_TILES], F32)
         two_rate = consts.tile([P, FEATURE_TILES], F32)
 
-        def prepare_vectors():
+        def prepare_gate_bias():
             nc.vector.tensor_scalar(
                 out=gate_bias[:],
-                in0=vectors[1][:],
+                in0=vectors[0][:],
                 scalar1=0.5,
                 scalar2=0.5 * math.log(3.0),
                 op0=ALU.mult,
                 op1=ALU.add,
             )
-            nc.vector.tensor_copy(out=in_bias[:], in_=vectors[0][:])
+
+        def prepare_in_bias():
+            nc.vector.tensor_copy(out=in_bias[:], in_=vectors[1][:])
+
+        def prepare_rates():
             nc.vector.reciprocal(out=inv_tau[:], in_=vectors[2][:])
             nc.vector.tensor_scalar_mul(out=neg_rate[:], in0=inv_tau[:], scalar1=-0.2 / 3.0)
             nc.vector.tensor_scalar_mul(out=two_rate[:], in0=inv_tau[:], scalar1=0.4 / 3.0)
@@ -154,113 +160,221 @@ def tile_liquidcell_pa_t_kernel(
         grouped = {}
         act = {}
 
-        def transpose_pair(index):
-            chunk, part = divmod(index, 4)
-            operand, pair = divmod(part, 2)
+        def transpose_in(chunk, operand):
             natural = (x_nat, h_nat)[operand][chunk]
-            if pair == 0:
-                grouped[(chunk, operand)] = stage.tile(
-                    [P, PACK * CHUNK], BF16, name="grouped%d" % operand, bufs=2 + operand, align_bytes=64
-                )
-            packed = grouped[(chunk, operand)]
-            words_t = psum.tile([P, 2, 2, P], F32, name="words_t", bufs=2)
-            for t in range(2):
-                words = natural[:, 2 * pair + t, :].bitcast(F32)
-                for u in range(2):
-                    nc.tensor.transpose(words_t[:, t, u, :], words[:, u:WORDS:2], ident_f32[:])
-            half = slice(pair * CHUNK, (pair + 1) * CHUNK)
-            nc.scalar.copy(
-                out=packed[:].bitcast(F32)[:, half].rearrange("p (t r u) -> p t r u", t=2, u=2),
-                in_=words_t[:].rearrange("p t u r -> p t r u"),
+            grouped[(chunk, operand)] = stage.tile(
+                [P, PACK * WIDEST], BF16, name="grouped%d" % operand, bufs=2 + operand, align_bytes=64
             )
-            if pair == 1:
-                codes = stage.tile([P, CHUNK], U32, name="codes%d" % operand, align_bytes=64)
-                scales = stage.tile([P, CHUNK], U8, name="scales%d" % operand, align_bytes=64)
-                nc.vector.quantize_mx(out=codes[:].bitcast(FP8X4), scales=scales[:], in_=packed[:])
-                act[(chunk, operand)] = (codes, scales)
+            packed = grouped[(chunk, operand)][:].bitcast(F32)
+            for pair in range(SIZES[chunk] // 2):
+                words_t = psum.tile([P, 2, 2, P], F32, name="words_t", bufs=2)
+                for t in range(2):
+                    words = natural[:, 2 * pair + t, :].bitcast(F32)
+                    for u in range(2):
+                        nc.tensor.transpose(words_t[:, t, u, :], words[:, u:WORDS:2], ident_f32[:])
+                half = slice(pair * 4 * P, (pair + 1) * 4 * P)
+                nc.scalar.copy(
+                    out=packed[:, half].rearrange("p (t r u) -> p t r u", t=2, u=2),
+                    in_=words_t[:].rearrange("p t u r -> p t r u"),
+                )
 
-        factors = {}
+        def quantize(chunk, operand):
+            width = SIZES[chunk] * P
+            codes = stage.tile([P, WIDEST], U32, name="codes%d" % operand, align_bytes=64)
+            scales = stage.tile([P, WIDEST], U8, name="scales%d" % operand, align_bytes=64)
+            nc.vector.quantize_mx(
+                out=codes[:, 0:width].bitcast(FP8X4),
+                scales=scales[:, 0:width],
+                in_=grouped[(chunk, operand)][:, 0 : PACK * width],
+            )
+            act[(chunk, operand)] = (codes, scales)
+
+        gates = {}
+        cells = {}
         step_t = {}
 
         def mx_pass(acc, weight, cols, chunk, operand, first):
+            width = SIZES[chunk] * P
             codes, scales = act[(chunk, operand)]
+            if weight < W_IN:
+                w_scale = tau_scales[:, weight, cols]
+            else:
+                w_scale = cell_scales[4:P, weight - W_IN, cols]
             nc.tensor.matmul_mx(
-                out=acc[:],
+                out=acc[:, 0:width],
                 lhsT=w_codes[:, weight, cols].bitcast(FP8X4),
-                lhsT_scale=w_scales[4 * weight : P, cols],
-                rhs=codes[:].bitcast(FP8X4),
-                rhs_scale=scales[:],
+                lhsT_scale=w_scale,
+                rhs=codes[:, 0:width].bitcast(FP8X4),
+                rhs_scale=scales[:, 0:width],
                 start=first,
                 stop=not first,
             )
 
-        def run_unit(unit):
-            chunk, j = divmod(unit, FEATURE_TILES)
+        def multiply_in(unit):
+            chunk, j = unit
+            width = SIZES[chunk] * P
             cols = slice(j * P, (j + 1) * P)
-            gate_sum = psum.tile([P, CHUNK], F32, tag="sums", bufs=4)
+            gate_sum = psum.tile([P, WIDEST], F32, tag="sums", bufs=4)
             mx_pass(gate_sum, W_TAU_X, cols, chunk, 0, True)
             mx_pass(gate_sum, W_TAU_H, cols, chunk, 1, False)
-            cell_sum = psum.tile([P, CHUNK], F32, tag="sums", bufs=4)
+            cell_sum = psum.tile([P, WIDEST], F32, tag="sums", bufs=4)
             mx_pass(cell_sum, W_IN, cols, chunk, 0, True)
             mx_pass(cell_sum, W_REC, cols, chunk, 1, False)
 
-            gate = work.tile([P, CHUNK], F32)
-            nc.scalar.activation(out=gate[:], in_=gate_sum[:], func=TANH, bias=gate_bias[:, j : j + 1], scale=0.5)
-            cell = work.tile([P, CHUNK], F32)
-            nc.scalar.activation(out=cell[:], in_=cell_sum[:], func=TANH, bias=in_bias[:, j : j + 1], scale=1.0)
-            if unit % 2 == 0:
-                nc.vector.tensor_scalar(
-                    out=gate[:],
-                    in0=gate[:],
-                    scalar1=neg_rate[:, j : j + 1],
-                    scalar2=two_rate[:, j : j + 1],
-                    op0=ALU.mult,
-                    op1=ALU.add,
-                )
-            else:
-                nc.scalar.activation(
-                    out=gate[:], in_=gate[:], func=IDENTITY, bias=two_rate[:, j : j + 1], scale=neg_rate[:, j : j + 1]
-                )
-            h_t = grouped[(chunk, 1)][:].rearrange("p (n j) -> p j n", j=PACK)[:, j, :]
-            nc.vector.tensor_tensor(out=cell[:], in0=cell[:], in1=h_t, op=ALU.subtract)
-            factors[unit] = (gate, cell)
-
-        def multiply_unit(unit):
-            chunk, j = divmod(unit, FEATURE_TILES)
-            gate, cell = factors[unit]
-            if j == 0:
-                step_t[chunk] = work.tile([P, FEATURE_TILES, CHUNK], F32, name="step_t")
-            nc.vector.tensor_tensor(out=step_t[chunk][:, j, :], in0=gate[:], in1=cell[:], op=ALU.mult)
-
-        def finish_rows(row_tile):
-            chunk, t = divmod(row_tile, CHUNK_TILES)
-            step_n = psum.tile([P, FEATURE_TILES, P], F32, name="step_n", bufs=2)
-            for j in range(FEATURE_TILES):
-                nc.tensor.transpose(step_n[:, j, :], step_t[chunk][:, j, t * P : (t + 1) * P], ident_f32[:])
-            result = work.tile([P, FEATURES], F32, bufs=4)
-            nc.vector.tensor_tensor(
-                out=result[:].rearrange("p (m j) -> p m j", j=FEATURE_TILES),
-                in0=step_n[:].rearrange("p j m -> p m j"),
-                in1=h_nat[chunk][:, t, :].rearrange("p (m j) -> p m j", j=FEATURE_TILES),
-                op=ALU.add,
+            gates[unit] = work.tile([P, WIDEST], F32, name="gate", bufs=4)
+            nc.scalar.activation(
+                out=gates[unit][:, 0:width], in_=gate_sum[:, 0:width], func=TANH, bias=gate_bias[:, j : j + 1], scale=0.5
             )
-            nc.sync.dma_start(out=out_rows[:, row_tile, :], in_=result[:])
+            cells[unit] = work.tile([P, WIDEST], F32, name="cell", bufs=4)
+            nc.scalar.activation(
+                out=cells[unit][:, 0:width], in_=cell_sum[:, 0:width], func=TANH, bias=in_bias[:, j : j + 1], scale=1.0
+            )
 
-        for step in range(UNITS + LEAD + LAG):
-            unit = step - LEAD
-            if step < UNITS:
-                transpose_pair(step)
-            if unit == -2:
-                arrange_scales()
-                arrange_codes(W_TAU_X)
-                arrange_codes(W_TAU_H)
-                prepare_vectors()
-            if unit == -1:
-                arrange_codes(W_IN)
-                arrange_codes(W_REC)
-            if 0 <= unit < UNITS:
-                run_unit(unit)
-            if 0 <= unit - LAG < ROW_TILES:
-                finish_rows(unit - LAG)
-            if 0 <= unit < UNITS:
-                multiply_unit(unit)
+        def rate_on_vector(unit):
+            chunk, j = unit
+            gate = gates[unit][:, 0 : SIZES[chunk] * P]
+            nc.vector.tensor_scalar(
+                out=gate,
+                in0=gate,
+                scalar1=neg_rate[:, j : j + 1],
+                scalar2=two_rate[:, j : j + 1],
+                op0=ALU.mult,
+                op1=ALU.add,
+            )
+
+        def rate_on_scalar(unit):
+            chunk, j = unit
+            gate = gates[unit][:, 0 : SIZES[chunk] * P]
+            nc.scalar.activation(
+                out=gate, in_=gate, func=IDENTITY, bias=two_rate[:, j : j + 1], scale=neg_rate[:, j : j + 1]
+            )
+
+        def subtract(unit):
+            chunk, j = unit
+            width = SIZES[chunk] * P
+            h_t = grouped[(chunk, 1)][:, 0 : PACK * width].rearrange("p (n j) -> p j n", j=PACK)[:, j, :]
+            cell = cells[unit][:, 0:width]
+            nc.vector.tensor_tensor(out=cell, in0=cell, in1=h_t, op=ALU.subtract)
+
+        def multiply_out(unit):
+            chunk, j = unit
+            width = SIZES[chunk] * P
+            if j == 0:
+                step_t[chunk] = work.tile([P, FEATURE_TILES, WIDEST], F32, name="step_t")
+            nc.vector.tensor_tensor(
+                out=step_t[chunk][:, j, 0:width],
+                in0=gates[unit][:, 0:width],
+                in1=cells[unit][:, 0:width],
+                op=ALU.mult,
+            )
+
+        back = {}
+
+        def transpose_back(row_tile, with_hidden):
+            chunk, t = row_tile
+            step_n = psum.tile([P, FEATURE_TILES, P], F32, name="step_n", bufs=2)
+            if with_hidden:
+                nc.tensor.matmul(
+                    step_n[:],
+                    lhsT=ident_bf16[:],
+                    rhs=h_nat[chunk][:, t, :].rearrange("p (m j) -> p j m", j=FEATURE_TILES),
+                    start=True,
+                    stop=False,
+                )
+            for j in range(FEATURE_TILES):
+                nc.tensor.matmul(
+                    step_n[:, j, :],
+                    lhsT=step_t[chunk][:, j, t * P : (t + 1) * P],
+                    rhs=ident_f32[:],
+                    is_transpose=True,
+                    start=not with_hidden,
+                    stop=not with_hidden or j == FEATURE_TILES - 1,
+                )
+            back[row_tile] = step_n
+
+        def finish(row_tile, with_hidden):
+            chunk, t = row_tile
+            result = work.tile([P, FEATURES], F32, bufs=4)
+            out_view = result[:].rearrange("p (m j) -> p m j", j=FEATURE_TILES)
+            step_view = back[row_tile][:].rearrange("p j m -> p m j")
+            if with_hidden:
+                nc.scalar.copy(out=out_view, in_=step_view)
+            else:
+                nc.vector.tensor_tensor(
+                    out=out_view,
+                    in0=step_view,
+                    in1=h_nat[chunk][:, t, :].rearrange("p (m j) -> p m j", j=FEATURE_TILES),
+                    op=ALU.add,
+                )
+            nc.sync.dma_start(out=out_rows[:, STARTS[chunk] + t, :], in_=result[:])
+
+        def back_rows(turn):
+            rows = []
+            for c in range(CHUNKS):
+                tiles = [(c, t) for t in range(SIZES[c])]
+                middle = (SIZES[c] + 1) // 2
+                if c == 0:
+                    places = [(2 * c + 3, tiles)]
+                elif c == CHUNKS - 1:
+                    places = [(2 * c + 2, tiles)]
+                elif c == CHUNKS - 2:
+                    places = [(2 * c + 2, tiles[:middle]), (2 * c + 3, tiles[middle:])]
+                else:
+                    places = [(2 * c + 3, tiles[:middle]), (2 * c + 4, tiles[middle:])]
+                for place, part in places:
+                    if place == turn:
+                        rows.extend(part)
+            return rows
+
+        turns = 2 * CHUNKS
+        transpose_in(0, 0)
+        transpose_in(0, 1)
+        quantize(0, 0)
+        arrange_gate(0)
+        quantize(0, 1)
+        prepare_gate_bias()
+        arrange_cell(0)
+        prepare_in_bias()
+        waiting = []
+        for turn in range(turns):
+            chunk, half = divmod(turn, 2)
+            units = [(chunk, 2 * half), (chunk, 2 * half + 1)]
+            rows = back_rows(turn)
+            matmuls_first = chunk == 0 or chunk == CHUNKS - 1
+            if matmuls_first:
+                for unit in units:
+                    multiply_in(unit)
+            if chunk + 1 < CHUNKS:
+                transpose_in(chunk + 1, half)
+            for place, row_tile in enumerate(rows):
+                with_hidden = row_tile[0] >= CHUNKS - 2 and row_tile[1] % 2 == 1
+                transpose_back(row_tile, with_hidden)
+                finish(row_tile, with_hidden)
+                if place == 0:
+                    while waiting:
+                        multiply_out(waiting.pop())
+            while waiting:
+                multiply_out(waiting.pop())
+            if not matmuls_first:
+                for unit in units:
+                    multiply_in(unit)
+            if turn == 0:
+                arrange_gate(1)
+                arrange_cell(1)
+                prepare_rates()
+            if turn % 4 < 3:
+                rate_on_vector(units[0])
+            else:
+                rate_on_scalar(units[0])
+            rate_on_scalar(units[1])
+            subtract(units[0])
+            if chunk + 1 < CHUNKS:
+                quantize(chunk + 1, half)
+            multiply_out(units[0])
+            subtract(units[1])
+            waiting.append(units[1])
+        multiply_out(waiting.pop())
+        for row_tile in back_rows(turns):
+            with_hidden = row_tile[1] % 2 == 1
+            transpose_back(row_tile, with_hidden)
+            finish(row_tile, with_hidden)

@@ -100,14 +100,13 @@ def tile_liquidcell_pa_t_kernel(
         ident_f32 = consts.tile([P, P], F32)
         make_identity(nc, ident_f32[:])
 
-        ident_bf16 = consts.tile([P, P], BF16)
-        make_identity(nc, ident_bf16[:])
-
         vectors = []
         for place, vec in enumerate((tau_adapt_b, W_in_b, tau_base)):
             vector = consts.tile([P, FEATURE_TILES], BF16, name="vector%d" % place)
             nc.gpsimd.dma_start(out=vector[:], in_=vec.rearrange("(p j) -> p j", j=FEATURE_TILES))
             vectors.append(vector)
+        ident_bf16 = consts.tile([P, P], BF16)
+        make_identity(nc, ident_bf16[:])
 
         zero_col = consts.tile([P, 1], F32)
         nc.vector.memset(zero_col[:], 0.0)
@@ -221,19 +220,29 @@ def tile_liquidcell_pa_t_kernel(
             mx_pass(cell_sum, W_IN, cols, chunk, 0, True)
             mx_pass(cell_sum, W_REC, cols, chunk, 1, False)
 
-            gates[unit] = work.tile([P, WIDEST], F32, name="gate", bufs=4)
+            half = (chunk, j // 2)
+            if j % 2 == 0:
+                gates[half] = work.tile([P, 2, WIDEST], F32, name="gate")
+                cells[half] = work.tile([P, 2, WIDEST], F32, name="cell")
             nc.scalar.activation(
-                out=gates[unit][:, 0:width], in_=gate_sum[:, 0:width], func=TANH, bias=gate_bias[:, j : j + 1], scale=0.5
+                out=gates[half][:, j % 2, 0:width],
+                in_=gate_sum[:, 0:width],
+                func=TANH,
+                bias=gate_bias[:, j : j + 1],
+                scale=0.5,
             )
-            cells[unit] = work.tile([P, WIDEST], F32, name="cell", bufs=4)
             nc.scalar.activation(
-                out=cells[unit][:, 0:width], in_=cell_sum[:, 0:width], func=TANH, bias=in_bias[:, j : j + 1], scale=1.0
+                out=cells[half][:, j % 2, 0:width],
+                in_=cell_sum[:, 0:width],
+                func=TANH,
+                bias=in_bias[:, j : j + 1],
+                scale=1.0,
             )
 
-        def rate_on_vector(unit):
+        def rate_on_gpsimd(unit):
             chunk, j = unit
-            gate = gates[unit][:, 0 : SIZES[chunk] * P]
-            nc.vector.tensor_scalar(
+            gate = gates[(chunk, j // 2)][:, j % 2, 0 : SIZES[chunk] * P]
+            nc.gpsimd.tensor_scalar(
                 out=gate,
                 in0=gate,
                 scalar1=neg_rate[:, j : j + 1],
@@ -244,27 +253,29 @@ def tile_liquidcell_pa_t_kernel(
 
         def rate_on_scalar(unit):
             chunk, j = unit
-            gate = gates[unit][:, 0 : SIZES[chunk] * P]
+            gate = gates[(chunk, j // 2)][:, j % 2, 0 : SIZES[chunk] * P]
             nc.scalar.activation(
                 out=gate, in_=gate, func=IDENTITY, bias=two_rate[:, j : j + 1], scale=neg_rate[:, j : j + 1]
             )
 
-        def subtract(unit):
-            chunk, j = unit
+        def subtract(half):
+            chunk, upper = half
             width = SIZES[chunk] * P
-            h_t = grouped[(chunk, 1)][:, 0 : PACK * width].rearrange("p (n j) -> p j n", j=PACK)[:, j, :]
-            cell = cells[unit][:, 0:width]
+            tiles = slice(2 * upper, 2 * upper + 2)
+            h_t = grouped[(chunk, 1)][:, 0 : PACK * width].rearrange("p (n j) -> p j n", j=PACK)[:, tiles, :]
+            cell = cells[half][:, :, 0:width]
             nc.vector.tensor_tensor(out=cell, in0=cell, in1=h_t, op=ALU.subtract)
 
-        def multiply_out(unit):
-            chunk, j = unit
+        def multiply_out(half):
+            chunk, upper = half
             width = SIZES[chunk] * P
-            if j == 0:
+            tiles = slice(2 * upper, 2 * upper + 2)
+            if upper == 0:
                 step_t[chunk] = work.tile([P, FEATURE_TILES, WIDEST], F32, name="step_t")
             nc.vector.tensor_tensor(
-                out=step_t[chunk][:, j, 0:width],
-                in0=gates[unit][:, 0:width],
-                in1=cells[unit][:, 0:width],
+                out=step_t[chunk][:, tiles, 0:width],
+                in0=gates[half][:, :, 0:width],
+                in1=cells[half][:, :, 0:width],
                 op=ALU.mult,
             )
 
@@ -308,73 +319,57 @@ def tile_liquidcell_pa_t_kernel(
                 )
             nc.sync.dma_start(out=out_rows[:, STARTS[chunk] + t, :], in_=result[:])
 
-        def back_rows(turn):
-            rows = []
-            for c in range(CHUNKS):
-                tiles = [(c, t) for t in range(SIZES[c])]
-                middle = (SIZES[c] + 1) // 2
-                if c == 0:
-                    places = [(2 * c + 3, tiles)]
-                elif c == CHUNKS - 1:
-                    places = [(2 * c + 2, tiles)]
-                elif c == CHUNKS - 2:
-                    places = [(2 * c + 2, tiles[:middle]), (2 * c + 3, tiles[middle:])]
-                else:
-                    places = [(2 * c + 3, tiles[:middle]), (2 * c + 4, tiles[middle:])]
-                for place, part in places:
-                    if place == turn:
-                        rows.extend(part)
-            return rows
-
-        turns = 2 * CHUNKS
         transpose_in(0, 0)
         transpose_in(0, 1)
-        quantize(0, 0)
         arrange_gate(0)
+        quantize(0, 0)
         quantize(0, 1)
         prepare_gate_bias()
         arrange_cell(0)
         prepare_in_bias()
         waiting = []
-        for turn in range(turns):
-            chunk, half = divmod(turn, 2)
-            units = [(chunk, 2 * half), (chunk, 2 * half + 1)]
-            rows = back_rows(turn)
+        rows = []
+        def take_product():
+            for half in waiting:
+                multiply_out(half)
+                if half[1] == 1:
+                    rows.extend([(half[0], t) for t in range(SIZES[half[0]])])
+            waiting.clear()
+
+        for turn in range(2 * CHUNKS):
+            chunk, upper = divmod(turn, 2)
+            units = [(chunk, 2 * upper), (chunk, 2 * upper + 1)]
+            tail = chunk >= CHUNKS - 2
+            going_back = rows[:4] if tail else rows[:2]
+            rows[:] = rows[len(going_back) :]
             matmuls_first = chunk == 0 or chunk == CHUNKS - 1
             if matmuls_first:
                 for unit in units:
                     multiply_in(unit)
             if chunk + 1 < CHUNKS:
-                transpose_in(chunk + 1, half)
-            for place, row_tile in enumerate(rows):
-                with_hidden = row_tile[0] >= CHUNKS - 2 and row_tile[1] % 2 == 1
-                transpose_back(row_tile, with_hidden)
-                finish(row_tile, with_hidden)
-                if place == 0:
-                    while waiting:
-                        multiply_out(waiting.pop())
-            while waiting:
-                multiply_out(waiting.pop())
-            if not matmuls_first:
-                for unit in units:
-                    multiply_in(unit)
+                transpose_in(chunk + 1, upper)
             if turn == 0:
                 arrange_gate(1)
                 arrange_cell(1)
                 prepare_rates()
-            if turn % 4 < 3:
-                rate_on_vector(units[0])
-            else:
-                rate_on_scalar(units[0])
+            for place, row_tile in enumerate(going_back):
+                with_hidden = row_tile[0] >= CHUNKS - 2 and row_tile[1] % 2 == 1
+                transpose_back(row_tile, with_hidden)
+                finish(row_tile, with_hidden)
+                if place == 0:
+                    take_product()
+            take_product()
+            if not matmuls_first:
+                for unit in units:
+                    multiply_in(unit)
+            rate_on_gpsimd(units[0])
             rate_on_scalar(units[1])
-            subtract(units[0])
             if chunk + 1 < CHUNKS:
-                quantize(chunk + 1, half)
-            multiply_out(units[0])
-            subtract(units[1])
-            waiting.append(units[1])
-        multiply_out(waiting.pop())
-        for row_tile in back_rows(turns):
+                quantize(chunk + 1, upper)
+            subtract((chunk, upper))
+            waiting.append((chunk, upper))
+        take_product()
+        for row_tile in rows:
             with_hidden = row_tile[1] % 2 == 1
             transpose_back(row_tile, with_hidden)
             finish(row_tile, with_hidden)

@@ -239,10 +239,10 @@ def tile_liquidcell_pa_t_kernel(
                 scale=1.0,
             )
 
-        def rate_on_gpsimd(unit):
+        def rate_on_vector(unit):
             chunk, j = unit
             gate = gates[(chunk, j // 2)][:, j % 2, 0 : SIZES[chunk] * P]
-            nc.gpsimd.tensor_scalar(
+            nc.vector.tensor_scalar(
                 out=gate,
                 in0=gate,
                 scalar1=neg_rate[:, j : j + 1],
@@ -336,11 +336,13 @@ def tile_liquidcell_pa_t_kernel(
                     rows.extend([(half[0], t) for t in range(SIZES[half[0]])])
             waiting.clear()
 
+        def on_scalar(row_tile):
+            return row_tile[1] == 3
+
         for turn in range(2 * CHUNKS):
             chunk, upper = divmod(turn, 2)
             units = [(chunk, 2 * upper), (chunk, 2 * upper + 1)]
-            tail = chunk >= CHUNKS - 2
-            going_back = rows[:4] if tail else rows[:2]
+            going_back = rows[:2]
             rows[:] = rows[len(going_back) :]
             matmuls_first = chunk == 0 or chunk == CHUNKS - 1
             if matmuls_first:
@@ -352,24 +354,23 @@ def tile_liquidcell_pa_t_kernel(
                 arrange_gate(1)
                 arrange_cell(1)
                 prepare_rates()
-            for place, row_tile in enumerate(going_back):
-                with_hidden = row_tile[0] >= CHUNKS - 2 and row_tile[1] % 2 == 1
-                transpose_back(row_tile, with_hidden)
-                finish(row_tile, with_hidden)
-                if place == 0:
-                    take_product()
+            for row_tile in going_back:
+                transpose_back(row_tile, on_scalar(row_tile))
+            for row_tile in going_back[:1]:
+                finish(row_tile, on_scalar(row_tile))
             take_product()
+            if chunk + 1 < CHUNKS:
+                quantize(chunk + 1, upper)
+            for row_tile in going_back[1:]:
+                finish(row_tile, on_scalar(row_tile))
             if not matmuls_first:
                 for unit in units:
                     multiply_in(unit)
-            rate_on_gpsimd(units[0])
+            rate_on_vector(units[0])
             rate_on_scalar(units[1])
-            if chunk + 1 < CHUNKS:
-                quantize(chunk + 1, upper)
             subtract((chunk, upper))
             waiting.append((chunk, upper))
         take_product()
         for row_tile in rows:
-            with_hidden = row_tile[1] % 2 == 1
-            transpose_back(row_tile, with_hidden)
-            finish(row_tile, with_hidden)
+            transpose_back(row_tile, on_scalar(row_tile))
+            finish(row_tile, on_scalar(row_tile))

@@ -11,7 +11,6 @@ U32 = mybir.dt.uint32
 I32 = mybir.dt.int32
 FP8X4 = mybir.dt.float8_e4m3fn_x4
 TANH = mybir.ActivationFunctionType.Tanh
-IDENTITY = mybir.ActivationFunctionType.Identity
 ALU = mybir.AluOpType
 
 P = 128
@@ -57,7 +56,7 @@ def tile_liquidcell_pa_t_kernel(
 
     with ExitStack() as stack:
         consts = stack.enter_context(tc.tile_pool(name="consts", bufs=1))
-        stage = stack.enter_context(tc.tile_pool(name="stage", bufs=2))
+        stage = stack.enter_context(tc.tile_pool(name="stage", bufs=3))
         work = stack.enter_context(tc.tile_pool(name="work", bufs=3))
         psum = stack.enter_context(tc.psum_pool(name="psum", bufs=1))
         stack.enter_context(tc.manual_schedule())
@@ -162,7 +161,7 @@ def tile_liquidcell_pa_t_kernel(
         def transpose_in(chunk, operand):
             natural = (x_nat, h_nat)[operand][chunk]
             grouped[(chunk, operand)] = stage.tile(
-                [P, PACK * WIDEST], BF16, name="grouped%d" % operand, bufs=2 + operand, align_bytes=64
+                [P, PACK * WIDEST], BF16, name="grouped%d" % operand, bufs=3 + operand, align_bytes=64
             )
             packed = grouped[(chunk, operand)][:].bitcast(F32)
             for pair in range(SIZES[chunk] // 2):
@@ -222,8 +221,8 @@ def tile_liquidcell_pa_t_kernel(
 
             half = (chunk, j // 2)
             if j % 2 == 0:
-                gates[half] = work.tile([P, 2, WIDEST], F32, name="gate")
-                cells[half] = work.tile([P, 2, WIDEST], F32, name="cell")
+                gates[half] = work.tile([P, 2, WIDEST], F32, name="gate", bufs=4)
+                cells[half] = work.tile([P, 2, WIDEST], F32, name="cell", bufs=4)
             nc.scalar.activation(
                 out=gates[half][:, j % 2, 0:width],
                 in_=gate_sum[:, 0:width],
@@ -249,13 +248,6 @@ def tile_liquidcell_pa_t_kernel(
                 scalar2=two_rate[:, j : j + 1],
                 op0=ALU.mult,
                 op1=ALU.add,
-            )
-
-        def rate_on_scalar(unit):
-            chunk, j = unit
-            gate = gates[(chunk, j // 2)][:, j % 2, 0 : SIZES[chunk] * P]
-            nc.scalar.activation(
-                out=gate, in_=gate, func=IDENTITY, bias=two_rate[:, j : j + 1], scale=neg_rate[:, j : j + 1]
             )
 
         def subtract(half):
@@ -305,7 +297,7 @@ def tile_liquidcell_pa_t_kernel(
 
         def finish(row_tile, with_hidden):
             chunk, t = row_tile
-            result = work.tile([P, FEATURES], F32, bufs=4)
+            result = work.tile([P, FEATURES], F32, bufs=8)
             out_view = result[:].rearrange("p (m j) -> p m j", j=FEATURE_TILES)
             step_view = back[row_tile][:].rearrange("p j m -> p m j")
             if with_hidden:
@@ -337,39 +329,38 @@ def tile_liquidcell_pa_t_kernel(
             waiting.clear()
 
         def on_scalar(row_tile):
-            return row_tile[1] == 3
+            return row_tile[1] % 2 == 0
 
+        operands = [(c, operand) for c in range(1, CHUNKS) for operand in range(2)]
         for turn in range(2 * CHUNKS):
             chunk, upper = divmod(turn, 2)
             units = [(chunk, 2 * upper), (chunk, 2 * upper + 1)]
             going_back = rows[:2]
             rows[:] = rows[len(going_back) :]
-            matmuls_first = chunk == 0 or chunk == CHUNKS - 1
-            if matmuls_first:
-                for unit in units:
-                    multiply_in(unit)
-            if chunk + 1 < CHUNKS:
-                transpose_in(chunk + 1, upper)
+            ahead = operands[:2] if turn == 1 else operands[:1]
+            operands[:] = operands[len(ahead) :]
+            if chunk > 0:
+                for operand in ahead:
+                    transpose_in(operand[0], operand[1])
+            for unit in units:
+                multiply_in(unit)
+            if chunk == 0:
+                for operand in ahead:
+                    transpose_in(operand[0], operand[1])
             if turn == 0:
                 arrange_gate(1)
                 arrange_cell(1)
                 prepare_rates()
-            for row_tile in going_back:
-                transpose_back(row_tile, on_scalar(row_tile))
-            for row_tile in going_back[:1]:
-                finish(row_tile, on_scalar(row_tile))
             take_product()
-            if chunk + 1 < CHUNKS:
-                quantize(chunk + 1, upper)
-            for row_tile in going_back[1:]:
-                finish(row_tile, on_scalar(row_tile))
-            if not matmuls_first:
-                for unit in units:
-                    multiply_in(unit)
-            rate_on_vector(units[0])
-            rate_on_scalar(units[1])
+            for operand in ahead:
+                quantize(operand[0], operand[1])
+            for unit in units:
+                rate_on_vector(unit)
             subtract((chunk, upper))
             waiting.append((chunk, upper))
+            for row_tile in going_back:
+                transpose_back(row_tile, on_scalar(row_tile))
+                finish(row_tile, on_scalar(row_tile))
         take_product()
         for row_tile in rows:
             transpose_back(row_tile, on_scalar(row_tile))

@@ -11,6 +11,7 @@ U32 = mybir.dt.uint32
 I32 = mybir.dt.int32
 FP8X4 = mybir.dt.float8_e4m3fn_x4
 TANH = mybir.ActivationFunctionType.Tanh
+IDENTITY = mybir.ActivationFunctionType.Identity
 ALU = mybir.AluOpType
 
 P = 128
@@ -104,8 +105,6 @@ def tile_liquidcell_pa_t_kernel(
             vector = consts.tile([P, FEATURE_TILES], BF16, name="vector%d" % place)
             nc.gpsimd.dma_start(out=vector[:], in_=vec.rearrange("(p j) -> p j", j=FEATURE_TILES))
             vectors.append(vector)
-        ident_bf16 = consts.tile([P, P], BF16)
-        make_identity(nc, ident_bf16[:])
 
         zero_col = consts.tile([P, 1], F32)
         nc.vector.memset(zero_col[:], 0.0)
@@ -250,6 +249,13 @@ def tile_liquidcell_pa_t_kernel(
                 op1=ALU.add,
             )
 
+        def rate_on_scalar(unit):
+            chunk, j = unit
+            gate = gates[(chunk, j // 2)][:, j % 2, 0 : SIZES[chunk] * P]
+            nc.scalar.activation(
+                out=gate, in_=gate, func=IDENTITY, bias=two_rate[:, j : j + 1], scale=neg_rate[:, j : j + 1]
+            )
+
         def subtract(half):
             chunk, upper = half
             width = SIZES[chunk] * P
@@ -273,42 +279,22 @@ def tile_liquidcell_pa_t_kernel(
 
         back = {}
 
-        def transpose_back(row_tile, with_hidden):
+        def transpose_back(row_tile):
             chunk, t = row_tile
             step_n = psum.tile([P, FEATURE_TILES, P], F32, name="step_n", bufs=2)
-            if with_hidden:
-                nc.tensor.matmul(
-                    step_n[:],
-                    lhsT=ident_bf16[:],
-                    rhs=h_nat[chunk][:, t, :].rearrange("p (m j) -> p j m", j=FEATURE_TILES),
-                    start=True,
-                    stop=False,
-                )
             for j in range(FEATURE_TILES):
-                nc.tensor.matmul(
-                    step_n[:, j, :],
-                    lhsT=step_t[chunk][:, j, t * P : (t + 1) * P],
-                    rhs=ident_f32[:],
-                    is_transpose=True,
-                    start=not with_hidden,
-                    stop=not with_hidden or j == FEATURE_TILES - 1,
-                )
+                nc.tensor.transpose(step_n[:, j, :], step_t[chunk][:, j, t * P : (t + 1) * P], ident_f32[:])
             back[row_tile] = step_n
 
-        def finish(row_tile, with_hidden):
+        def finish(row_tile):
             chunk, t = row_tile
             result = work.tile([P, FEATURES], F32, bufs=8)
-            out_view = result[:].rearrange("p (m j) -> p m j", j=FEATURE_TILES)
-            step_view = back[row_tile][:].rearrange("p j m -> p m j")
-            if with_hidden:
-                nc.scalar.copy(out=out_view, in_=step_view)
-            else:
-                nc.vector.tensor_tensor(
-                    out=out_view,
-                    in0=step_view,
-                    in1=h_nat[chunk][:, t, :].rearrange("p (m j) -> p m j", j=FEATURE_TILES),
-                    op=ALU.add,
-                )
+            nc.vector.tensor_tensor(
+                out=result[:].rearrange("p (m j) -> p m j", j=FEATURE_TILES),
+                in0=back[row_tile][:].rearrange("p j m -> p m j"),
+                in1=h_nat[chunk][:, t, :].rearrange("p (m j) -> p m j", j=FEATURE_TILES),
+                op=ALU.add,
+            )
             nc.sync.dma_start(out=out_rows[:, STARTS[chunk] + t, :], in_=result[:])
 
         transpose_in(0, 0)
@@ -328,40 +314,39 @@ def tile_liquidcell_pa_t_kernel(
                     rows.extend([(half[0], t) for t in range(SIZES[half[0]])])
             waiting.clear()
 
-        def on_scalar(row_tile):
-            return row_tile[1] % 2 == 0
-
-        operands = [(c, operand) for c in range(1, CHUNKS) for operand in range(2)]
         for turn in range(2 * CHUNKS):
             chunk, upper = divmod(turn, 2)
             units = [(chunk, 2 * upper), (chunk, 2 * upper + 1)]
             going_back = rows[:2]
-            rows[:] = rows[len(going_back) :]
-            ahead = operands[:2] if turn == 1 else operands[:1]
-            operands[:] = operands[len(ahead) :]
-            if chunk > 0:
-                for operand in ahead:
-                    transpose_in(operand[0], operand[1])
+            rows[:] = rows[2:]
+            ahead = chunk + 1 < CHUNKS
+            if ahead and chunk > 0:
+                transpose_in(chunk + 1, upper)
             for unit in units:
                 multiply_in(unit)
-            if chunk == 0:
-                for operand in ahead:
-                    transpose_in(operand[0], operand[1])
+            if ahead and chunk == 0:
+                transpose_in(chunk + 1, upper)
             if turn == 0:
                 arrange_gate(1)
                 arrange_cell(1)
                 prepare_rates()
             take_product()
-            for operand in ahead:
-                quantize(operand[0], operand[1])
+            if ahead:
+                quantize(chunk + 1, upper)
+            for row_tile in going_back[:1]:
+                transpose_back(row_tile)
+                finish(row_tile)
             for unit in units:
-                rate_on_vector(unit)
+                if unit[1] == 0:
+                    rate_on_vector(unit)
+                else:
+                    rate_on_scalar(unit)
             subtract((chunk, upper))
             waiting.append((chunk, upper))
-            for row_tile in going_back:
-                transpose_back(row_tile, on_scalar(row_tile))
-                finish(row_tile, on_scalar(row_tile))
+            for row_tile in going_back[1:]:
+                transpose_back(row_tile)
+                finish(row_tile)
         take_product()
         for row_tile in rows:
-            transpose_back(row_tile, on_scalar(row_tile))
-            finish(row_tile, on_scalar(row_tile))
+            transpose_back(row_tile)
+            finish(row_tile)

@@ -71,9 +71,9 @@ def tile_liquidcell_pa_t_kernel(
         load(x_nat, x_rows, 0)
         load(h_nat, h_rows, 0)
 
-        tau_scales_raw = consts.tile([P, 2, FEATURES], U8, align_bytes=64)
+        tau_scales_raw = consts.tile([P, 2, FEATURES], U8, align_bytes=256)
         nc.vector.memset(tau_scales_raw[:].rearrange("p w n -> p (w n)").bitcast(I32), 0)
-        cell_scales_raw = consts.tile([P, 2, FEATURES], U8, align_bytes=64)
+        cell_scales_raw = consts.tile([P, 2, FEATURES], U8, align_bytes=256)
         nc.vector.memset(cell_scales_raw[:].rearrange("p w n -> p (w n)").bitcast(I32), 0)
         quads = [(slice(4 * q, 4 * q + 4), slice(32 * q, 32 * q + 4)) for q in range(4)]
         for rows, parts in quads:
@@ -82,7 +82,7 @@ def tile_liquidcell_pa_t_kernel(
                 in_=tau_adapt_w_scales[:, rows, :].rearrange("g r n -> r g n").bitcast(I32),
             )
 
-        raw_codes = consts.tile([P, 4, FEATURES], I32, align_bytes=64)
+        raw_codes = consts.tile([P, 4, FEATURES], I32, align_bytes=256)
         nc.sync.dma_start(
             out=raw_codes[:, W_TAU_X : W_TAU_H + 1, :],
             in_=tau_adapt_w_words.rearrange("g p n t -> p g (n t)").bitcast(I32),
@@ -111,9 +111,9 @@ def tile_liquidcell_pa_t_kernel(
         warm_col = consts.tile([P, 1], F32)
         nc.scalar.activation(out=warm_col[:], in_=zero_col[:], func=TANH)
 
-        tau_scales = consts.tile([P, 2, FEATURES], U8, align_bytes=64)
-        cell_scales = consts.tile([P, 2, FEATURES], U8, align_bytes=64)
-        w_codes = consts.tile([P, 4, FEATURES], I32, align_bytes=64)
+        tau_scales = consts.tile([P, 2, FEATURES], U8, align_bytes=256)
+        cell_scales = consts.tile([P, 2, FEATURES], U8, align_bytes=256)
+        w_codes = consts.tile([P, 4, FEATURES], I32, align_bytes=256)
 
         def arrange(out, in_, half):
             tiles = slice(2 * half, 2 * half + 2)
@@ -160,7 +160,7 @@ def tile_liquidcell_pa_t_kernel(
         def transpose_in(chunk, operand):
             natural = (x_nat, h_nat)[operand][chunk]
             grouped[(chunk, operand)] = stage.tile(
-                [P, PACK * WIDEST], BF16, name="grouped%d" % operand, bufs=3 + operand, align_bytes=64
+                [P, PACK * WIDEST], BF16, name="grouped%d" % operand, bufs=3 + operand, align_bytes=256
             )
             packed = grouped[(chunk, operand)][:].bitcast(F32)
             for pair in range(SIZES[chunk] // 2):
@@ -177,8 +177,8 @@ def tile_liquidcell_pa_t_kernel(
 
         def quantize(chunk, operand):
             width = SIZES[chunk] * P
-            codes = stage.tile([P, WIDEST], U32, name="codes%d" % operand, align_bytes=64)
-            scales = stage.tile([P, WIDEST], U8, name="scales%d" % operand, align_bytes=64)
+            codes = stage.tile([P, WIDEST], U32, name="codes%d" % operand, align_bytes=256)
+            scales = stage.tile([P, WIDEST], U8, name="scales%d" % operand, align_bytes=256)
             nc.vector.quantize_mx(
                 out=codes[:, 0:width].bitcast(FP8X4),
                 scales=scales[:, 0:width],

@@ -26,6 +26,8 @@ CHUNKS = len(SIZES)
 WIDEST = max(SIZES) * P
 FEATURE_TILES = FEATURES // P
 
+SPLIT = (CHUNKS - 2,)
+
 W_TAU_X = 0
 W_TAU_H = 1
 W_IN = 2
@@ -65,15 +67,15 @@ def tile_liquidcell_pa_t_kernel(
         x_nat = [consts.tile([P, SIZES[c], FEATURES], BF16, name="x_nat%d" % c) for c in range(CHUNKS)]
         h_nat = [consts.tile([P, SIZES[c], FEATURES], BF16, name="h_nat%d" % c) for c in range(CHUNKS)]
 
-        def load(natural, rows, c):
-            nc.sync.dma_start(out=natural[c][:], in_=rows[:, STARTS[c] : STARTS[c] + SIZES[c], :])
+        def load(natural, rows, c, queue):
+            queue.dma_start(out=natural[c][:], in_=rows[:, STARTS[c] : STARTS[c] + SIZES[c], :])
 
-        load(x_nat, x_rows, 0)
-        load(h_nat, h_rows, 0)
+        load(x_nat, x_rows, 0, nc.sync)
+        load(h_nat, h_rows, 0, nc.sync)
 
-        tau_scales_raw = consts.tile([P, 2, FEATURES], U8, align_bytes=256)
+        tau_scales_raw = consts.tile([P, 2, FEATURES], U8, align_bytes=64)
         nc.vector.memset(tau_scales_raw[:].rearrange("p w n -> p (w n)").bitcast(I32), 0)
-        cell_scales_raw = consts.tile([P, 2, FEATURES], U8, align_bytes=256)
+        cell_scales_raw = consts.tile([P, 2, FEATURES], U8, align_bytes=64)
         nc.vector.memset(cell_scales_raw[:].rearrange("p w n -> p (w n)").bitcast(I32), 0)
         quads = [(slice(4 * q, 4 * q + 4), slice(32 * q, 32 * q + 4)) for q in range(4)]
         for rows, parts in quads:
@@ -82,38 +84,51 @@ def tile_liquidcell_pa_t_kernel(
                 in_=tau_adapt_w_scales[:, rows, :].rearrange("g r n -> r g n").bitcast(I32),
             )
 
-        raw_codes = consts.tile([P, 4, FEATURES], I32, align_bytes=256)
+        raw_codes = consts.tile([P, 4, FEATURES], I32, align_bytes=64)
         nc.sync.dma_start(
             out=raw_codes[:, W_TAU_X : W_TAU_H + 1, :],
             in_=tau_adapt_w_words.rearrange("g p n t -> p g (n t)").bitcast(I32),
         )
+        def load_vector(vec, name):
+            vector = consts.tile([P, FEATURE_TILES], BF16, name=name)
+            nc.sync.dma_start(out=vector[:], in_=vec.rearrange("(p j) -> p j", j=FEATURE_TILES))
+            return vector
+
+        gate_vector = load_vector(tau_adapt_b, "gate_vector")
+        nc.sync.dma_start(out=raw_codes[:, W_IN, :], in_=W_in_w_words[0].rearrange("p n t -> p (n t)").bitcast(I32))
+        nc.sync.dma_start(out=raw_codes[:, W_REC, :], in_=W_rec_words[0].rearrange("p n t -> p (n t)").bitcast(I32))
+        in_vector = load_vector(W_in_b, "in_vector")
+        tau_vector = load_vector(tau_base, "tau_vector")
         for rows, parts in quads:
             lower = slice(parts.start + 4, parts.stop + 4)
             nc.sync.dma_start(out=cell_scales_raw[lower, 0, :].bitcast(I32), in_=W_in_w_scales[0, rows, :].bitcast(I32))
             nc.sync.dma_start(out=cell_scales_raw[lower, 1, :].bitcast(I32), in_=W_rec_scales[0, rows, :].bitcast(I32))
-        nc.sync.dma_start(out=raw_codes[:, W_IN, :], in_=W_in_w_words[0].rearrange("p n t -> p (n t)").bitcast(I32))
-        nc.sync.dma_start(out=raw_codes[:, W_REC, :], in_=W_rec_words[0].rearrange("p n t -> p (n t)").bitcast(I32))
-        for c in range(1, CHUNKS):
-            load(x_nat, x_rows, c)
-            load(h_nat, h_rows, c)
+        for c in range(2, CHUNKS):
+            load(x_nat, x_rows, c, nc.sync)
+            load(h_nat, h_rows, c, nc.sync)
 
         ident_f32 = consts.tile([P, P], F32)
         make_identity(nc, ident_f32[:])
 
-        vectors = []
-        for place, vec in enumerate((tau_adapt_b, W_in_b, tau_base)):
-            vector = consts.tile([P, FEATURE_TILES], BF16, name="vector%d" % place)
-            nc.gpsimd.dma_start(out=vector[:], in_=vec.rearrange("(p j) -> p j", j=FEATURE_TILES))
-            vectors.append(vector)
+        load(x_nat, x_rows, 1, nc.gpsimd)
+        load(h_nat, h_rows, 1, nc.gpsimd)
+
+        zeros = consts.tile([P, 4 * P], BF16)
+        nc.vector.memset(zeros[:], 0.0)
+
+        def keep_warm(count):
+            for repeat in range(count):
+                unread = psum.tile([P, 4 * P], F32, tag="step_n", bufs=2)
+                nc.tensor.matmul(unread[:], lhsT=zeros[:, 0:P], rhs=zeros[:], start=True, stop=True)
 
         zero_col = consts.tile([P, 1], F32)
         nc.vector.memset(zero_col[:], 0.0)
         warm_col = consts.tile([P, 1], F32)
         nc.scalar.activation(out=warm_col[:], in_=zero_col[:], func=TANH)
 
-        tau_scales = consts.tile([P, 2, FEATURES], U8, align_bytes=256)
-        cell_scales = consts.tile([P, 2, FEATURES], U8, align_bytes=256)
-        w_codes = consts.tile([P, 4, FEATURES], I32, align_bytes=256)
+        tau_scales = consts.tile([P, 2, FEATURES], U8, align_bytes=64)
+        cell_scales = consts.tile([P, 2, FEATURES], U8, align_bytes=64)
+        w_codes = consts.tile([P, 4, FEATURES], I32, align_bytes=64)
 
         def arrange(out, in_, half):
             tiles = slice(2 * half, 2 * half + 2)
@@ -130,16 +145,16 @@ def tile_liquidcell_pa_t_kernel(
             arrange(cell_scales[:], cell_scales_raw[:], half)
             arrange(w_codes[:, W_IN : W_REC + 1, :], raw_codes[:, W_IN : W_REC + 1, :], half)
 
-        in_bias = consts.tile([P, FEATURE_TILES], F32)
+        neg_in_bias = consts.tile([P, FEATURE_TILES], F32)
         gate_bias = consts.tile([P, FEATURE_TILES], F32)
         inv_tau = consts.tile([P, FEATURE_TILES], F32)
-        neg_rate = consts.tile([P, FEATURE_TILES], F32)
-        two_rate = consts.tile([P, FEATURE_TILES], F32)
+        rate = consts.tile([P, FEATURE_TILES], F32)
+        neg_two_rate = consts.tile([P, FEATURE_TILES], F32)
 
         def prepare_gate_bias():
             nc.vector.tensor_scalar(
                 out=gate_bias[:],
-                in0=vectors[0][:],
+                in0=gate_vector[:],
                 scalar1=0.5,
                 scalar2=0.5 * math.log(3.0),
                 op0=ALU.mult,
@@ -147,12 +162,12 @@ def tile_liquidcell_pa_t_kernel(
             )
 
         def prepare_in_bias():
-            nc.vector.tensor_copy(out=in_bias[:], in_=vectors[1][:])
+            nc.vector.tensor_scalar_mul(out=neg_in_bias[:], in0=in_vector[:], scalar1=-1.0)
 
         def prepare_rates():
-            nc.vector.reciprocal(out=inv_tau[:], in_=vectors[2][:])
-            nc.vector.tensor_scalar_mul(out=neg_rate[:], in0=inv_tau[:], scalar1=-0.2 / 3.0)
-            nc.vector.tensor_scalar_mul(out=two_rate[:], in0=inv_tau[:], scalar1=0.4 / 3.0)
+            nc.vector.reciprocal(out=inv_tau[:], in_=tau_vector[:])
+            nc.vector.tensor_scalar_mul(out=rate[:], in0=inv_tau[:], scalar1=0.2 / 3.0)
+            nc.vector.tensor_scalar_mul(out=neg_two_rate[:], in0=inv_tau[:], scalar1=-0.4 / 3.0)
 
         grouped = {}
         act = {}
@@ -160,7 +175,7 @@ def tile_liquidcell_pa_t_kernel(
         def transpose_in(chunk, operand):
             natural = (x_nat, h_nat)[operand][chunk]
             grouped[(chunk, operand)] = stage.tile(
-                [P, PACK * WIDEST], BF16, name="grouped%d" % operand, bufs=3 + operand, align_bytes=256
+                [P, PACK * WIDEST], BF16, name="grouped%d" % operand, bufs=3 + operand, align_bytes=64
             )
             packed = grouped[(chunk, operand)][:].bitcast(F32)
             for pair in range(SIZES[chunk] // 2):
@@ -177,8 +192,8 @@ def tile_liquidcell_pa_t_kernel(
 
         def quantize(chunk, operand):
             width = SIZES[chunk] * P
-            codes = stage.tile([P, WIDEST], U32, name="codes%d" % operand, align_bytes=256)
-            scales = stage.tile([P, WIDEST], U8, name="scales%d" % operand, align_bytes=256)
+            codes = stage.tile([P, WIDEST], U32, name="codes%d" % operand, align_bytes=64)
+            scales = stage.tile([P, WIDEST], U8, name="scales%d" % operand, align_bytes=64)
             nc.vector.quantize_mx(
                 out=codes[:, 0:width].bitcast(FP8X4),
                 scales=scales[:, 0:width],
@@ -189,6 +204,7 @@ def tile_liquidcell_pa_t_kernel(
         gates = {}
         cells = {}
         step_t = {}
+        kept_t = {}
 
         def mx_pass(acc, weight, cols, chunk, operand, first):
             width = SIZES[chunk] * P
@@ -207,21 +223,16 @@ def tile_liquidcell_pa_t_kernel(
                 stop=not first,
             )
 
-        def multiply_in(unit):
+        def gate_in(unit):
             chunk, j = unit
             width = SIZES[chunk] * P
             cols = slice(j * P, (j + 1) * P)
-            gate_sum = psum.tile([P, WIDEST], F32, tag="sums", bufs=4)
-            mx_pass(gate_sum, W_TAU_X, cols, chunk, 0, True)
-            mx_pass(gate_sum, W_TAU_H, cols, chunk, 1, False)
-            cell_sum = psum.tile([P, WIDEST], F32, tag="sums", bufs=4)
-            mx_pass(cell_sum, W_IN, cols, chunk, 0, True)
-            mx_pass(cell_sum, W_REC, cols, chunk, 1, False)
-
             half = (chunk, j // 2)
             if j % 2 == 0:
                 gates[half] = work.tile([P, 2, WIDEST], F32, name="gate", bufs=4)
-                cells[half] = work.tile([P, 2, WIDEST], F32, name="cell", bufs=4)
+            gate_sum = psum.tile([P, WIDEST], F32, tag="sums", bufs=4)
+            mx_pass(gate_sum, W_TAU_X, cols, chunk, 0, True)
+            mx_pass(gate_sum, W_TAU_H, cols, chunk, 1, False)
             nc.scalar.activation(
                 out=gates[half][:, j % 2, 0:width],
                 in_=gate_sum[:, 0:width],
@@ -229,12 +240,23 @@ def tile_liquidcell_pa_t_kernel(
                 bias=gate_bias[:, j : j + 1],
                 scale=0.5,
             )
+
+        def cell_in(unit):
+            chunk, j = unit
+            width = SIZES[chunk] * P
+            cols = slice(j * P, (j + 1) * P)
+            half = (chunk, j // 2)
+            if j % 2 == 0:
+                cells[half] = work.tile([P, 2, WIDEST], F32, name="cell", bufs=4)
+            cell_sum = psum.tile([P, WIDEST], F32, tag="sums", bufs=4)
+            mx_pass(cell_sum, W_IN, cols, chunk, 0, True)
+            mx_pass(cell_sum, W_REC, cols, chunk, 1, False)
             nc.scalar.activation(
                 out=cells[half][:, j % 2, 0:width],
                 in_=cell_sum[:, 0:width],
                 func=TANH,
-                bias=in_bias[:, j : j + 1],
-                scale=1.0,
+                bias=neg_in_bias[:, j : j + 1],
+                scale=-1.0,
             )
 
         def rate_on_vector(unit):
@@ -243,8 +265,8 @@ def tile_liquidcell_pa_t_kernel(
             nc.vector.tensor_scalar(
                 out=gate,
                 in0=gate,
-                scalar1=neg_rate[:, j : j + 1],
-                scalar2=two_rate[:, j : j + 1],
+                scalar1=rate[:, j : j + 1],
+                scalar2=neg_two_rate[:, j : j + 1],
                 op0=ALU.mult,
                 op1=ALU.add,
             )
@@ -253,16 +275,28 @@ def tile_liquidcell_pa_t_kernel(
             chunk, j = unit
             gate = gates[(chunk, j // 2)][:, j % 2, 0 : SIZES[chunk] * P]
             nc.scalar.activation(
-                out=gate, in_=gate, func=IDENTITY, bias=two_rate[:, j : j + 1], scale=neg_rate[:, j : j + 1]
+                out=gate, in_=gate, func=IDENTITY, bias=neg_two_rate[:, j : j + 1], scale=rate[:, j : j + 1]
             )
 
-        def subtract(half):
+        def meet_hidden(half):
             chunk, upper = half
             width = SIZES[chunk] * P
             tiles = slice(2 * upper, 2 * upper + 2)
             h_t = grouped[(chunk, 1)][:, 0 : PACK * width].rearrange("p (n j) -> p j n", j=PACK)[:, tiles, :]
             cell = cells[half][:, :, 0:width]
-            nc.vector.tensor_tensor(out=cell, in0=cell, in1=h_t, op=ALU.subtract)
+            if chunk in SPLIT:
+                if upper == 0:
+                    kept_t[chunk] = work.tile([P, FEATURE_TILES, WIDEST], F32, name="kept_t", bufs=1)
+                nc.vector.scalar_tensor_tensor(
+                    out=kept_t[chunk][:, tiles, 0:width],
+                    in0=gates[half][:, :, 0:width],
+                    scalar=1.0,
+                    in1=h_t,
+                    op0=ALU.add,
+                    op1=ALU.mult,
+                )
+            else:
+                nc.vector.tensor_tensor(out=cell, in0=cell, in1=h_t, op=ALU.add)
 
         def multiply_out(half):
             chunk, upper = half
@@ -281,30 +315,61 @@ def tile_liquidcell_pa_t_kernel(
 
         def transpose_back(row_tile):
             chunk, t = row_tile
+            rows = slice(t * P, (t + 1) * P)
             step_n = psum.tile([P, FEATURE_TILES, P], F32, name="step_n", bufs=2)
             for j in range(FEATURE_TILES):
-                nc.tensor.transpose(step_n[:, j, :], step_t[chunk][:, j, t * P : (t + 1) * P], ident_f32[:])
+                if chunk in SPLIT:
+                    parts = (step_t[chunk], kept_t[chunk])
+                else:
+                    parts = (step_t[chunk],)
+                for part in parts:
+                    nc.tensor.matmul(
+                        step_n[:, j, :],
+                        lhsT=part[:, j, rows],
+                        rhs=ident_f32[:],
+                        is_transpose=True,
+                        start=part is parts[0],
+                        stop=part is parts[-1],
+                    )
             back[row_tile] = step_n
 
         def finish(row_tile):
             chunk, t = row_tile
             result = work.tile([P, FEATURES], F32, bufs=8)
-            nc.vector.tensor_tensor(
-                out=result[:].rearrange("p (m j) -> p m j", j=FEATURE_TILES),
-                in0=back[row_tile][:].rearrange("p j m -> p m j"),
-                in1=h_nat[chunk][:, t, :].rearrange("p (m j) -> p m j", j=FEATURE_TILES),
-                op=ALU.add,
-            )
+            out_view = result[:].rearrange("p (m j) -> p m j", j=FEATURE_TILES)
+            step_view = back[row_tile][:].rearrange("p j m -> p m j")
+            if chunk in SPLIT:
+                nc.scalar.copy(out=out_view, in_=step_view)
+            else:
+                nc.vector.tensor_tensor(
+                    out=out_view,
+                    in0=step_view,
+                    in1=h_nat[chunk][:, t, :].rearrange("p (m j) -> p m j", j=FEATURE_TILES),
+                    op=ALU.add,
+                )
             nc.sync.dma_start(out=out_rows[:, STARTS[chunk] + t, :], in_=result[:])
 
+        keep_warm(2)
         transpose_in(0, 0)
         transpose_in(0, 1)
+        keep_warm(4)
         arrange_gate(0)
         quantize(0, 0)
         quantize(0, 1)
         prepare_gate_bias()
-        arrange_cell(0)
-        prepare_in_bias()
+        arrange_gate(1)
+        for upper in range(2):
+            for j in range(2 * upper, 2 * upper + 2):
+                gate_in((0, j))
+            transpose_in(1, upper)
+            if upper == 0:
+                quantize(1, 0)
+                arrange_cell(0)
+                prepare_in_bias()
+            else:
+                arrange_cell(1)
+                quantize(1, 1)
+        prepare_rates()
         waiting = []
         rows = []
         def take_product():
@@ -323,15 +388,11 @@ def tile_liquidcell_pa_t_kernel(
             if ahead and chunk > 0:
                 transpose_in(chunk + 1, upper)
             for unit in units:
-                multiply_in(unit)
-            if ahead and chunk == 0:
-                transpose_in(chunk + 1, upper)
-            if turn == 0:
-                arrange_gate(1)
-                arrange_cell(1)
-                prepare_rates()
+                if chunk > 0:
+                    gate_in(unit)
+                cell_in(unit)
             take_product()
-            if ahead:
+            if ahead and chunk > 0:
                 quantize(chunk + 1, upper)
             for row_tile in going_back[:1]:
                 transpose_back(row_tile)
@@ -341,7 +402,7 @@ def tile_liquidcell_pa_t_kernel(
                     rate_on_vector(unit)
                 else:
                     rate_on_scalar(unit)
-            subtract((chunk, upper))
+            meet_hidden((chunk, upper))
             waiting.append((chunk, upper))
             for row_tile in going_back[1:]:
                 transpose_back(row_tile)

@@ -313,10 +313,10 @@ def tile_liquidcell_pa_t_kernel(
 
         back = {}
 
-        def transpose_back(row_tile):
+        def transpose_back(row_tile, tag, bufs):
             chunk, t = row_tile
             rows = slice(t * P, (t + 1) * P)
-            step_n = psum.tile([P, FEATURE_TILES, P], F32, name="step_n", bufs=2)
+            step_n = psum.tile([P, FEATURE_TILES, P], F32, tag=tag, bufs=bufs)
             for j in range(FEATURE_TILES):
                 if chunk in SPLIT:
                     parts = (step_t[chunk], kept_t[chunk])
@@ -395,7 +395,7 @@ def tile_liquidcell_pa_t_kernel(
             if ahead and chunk > 0:
                 quantize(chunk + 1, upper)
             for row_tile in going_back[:1]:
-                transpose_back(row_tile)
+                transpose_back(row_tile, "step_n", 2)
                 finish(row_tile)
             for unit in units:
                 if unit[1] == 0:
@@ -405,9 +405,12 @@ def tile_liquidcell_pa_t_kernel(
             meet_hidden((chunk, upper))
             waiting.append((chunk, upper))
             for row_tile in going_back[1:]:
-                transpose_back(row_tile)
+                if turn < 2 * CHUNKS - 3:
+                    transpose_back(row_tile, "step_n", 2)
+                else:
+                    transpose_back(row_tile, "words_t", 2)
                 finish(row_tile)
         take_product()
         for row_tile in rows:
-            transpose_back(row_tile)
+            transpose_back(row_tile, "sums", 4)
             finish(row_tile)

@@ -97,12 +97,12 @@ def tile_liquidcell_pa_t_kernel(
         gate_vector = load_vector(tau_adapt_b, "gate_vector")
         nc.sync.dma_start(out=raw_codes[:, W_IN, :], in_=W_in_w_words[0].rearrange("p n t -> p (n t)").bitcast(I32))
         nc.sync.dma_start(out=raw_codes[:, W_REC, :], in_=W_rec_words[0].rearrange("p n t -> p (n t)").bitcast(I32))
-        in_vector = load_vector(W_in_b, "in_vector")
-        tau_vector = load_vector(tau_base, "tau_vector")
         for rows, parts in quads:
             lower = slice(parts.start + 4, parts.stop + 4)
             nc.sync.dma_start(out=cell_scales_raw[lower, 0, :].bitcast(I32), in_=W_in_w_scales[0, rows, :].bitcast(I32))
             nc.sync.dma_start(out=cell_scales_raw[lower, 1, :].bitcast(I32), in_=W_rec_scales[0, rows, :].bitcast(I32))
+        in_vector = load_vector(W_in_b, "in_vector")
+        tau_vector = load_vector(tau_base, "tau_vector")
         for c in range(2, CHUNKS):
             load(x_nat, x_rows, c, nc.sync)
             load(h_nat, h_rows, c, nc.sync)
@@ -362,14 +362,12 @@ def tile_liquidcell_pa_t_kernel(
             for j in range(2 * upper, 2 * upper + 2):
                 gate_in((0, j))
             transpose_in(1, upper)
-            if upper == 0:
-                quantize(1, 0)
-                arrange_cell(0)
-                prepare_in_bias()
-            else:
-                arrange_cell(1)
-                quantize(1, 1)
+        arrange_cell(0)
+        arrange_cell(1)
+        prepare_in_bias()
         prepare_rates()
+        quantize(1, 0)
+        quantize(1, 1)
         waiting = []
         rows = []
         def take_product():

@@ -33,6 +33,8 @@ W_TAU_H = 1
 W_IN = 2
 W_REC = 3
 
+EARLY = 3
+
 FLOPS = 4 * 2 * BATCH * FEATURES * FEATURES
 
 
@@ -271,6 +273,13 @@ def tile_liquidcell_pa_t_kernel(
                 op1=ALU.add,
             )
 
+        def vector_rates(chunk):
+            if chunk < EARLY:
+                return (0, 2)
+            if chunk < CHUNKS - 1:
+                return (0,)
+            return ()
+
         def rate_on_scalar(unit):
             chunk, j = unit
             gate = gates[(chunk, j // 2)][:, j % 2, 0 : SIZES[chunk] * P]
@@ -389,24 +398,28 @@ def tile_liquidcell_pa_t_kernel(
                 if chunk > 0:
                     gate_in(unit)
                 cell_in(unit)
-            take_product()
+            if turn < 2 * CHUNKS - 1:
+                take_product()
             if ahead and chunk > 0:
                 quantize(chunk + 1, upper)
-            for row_tile in going_back[:1]:
-                transpose_back(row_tile, "step_n", 2)
+            first = going_back if turn >= 2 * CHUNKS - 4 else going_back[:1]
+            for row_tile in first:
+                if turn < 2 * CHUNKS - 3 or row_tile is first[0]:
+                    transpose_back(row_tile, "step_n", 2)
+                else:
+                    transpose_back(row_tile, "words_t", 2)
                 finish(row_tile)
             for unit in units:
-                if unit[1] == 0:
+                if unit[1] in vector_rates(chunk):
                     rate_on_vector(unit)
                 else:
                     rate_on_scalar(unit)
             meet_hidden((chunk, upper))
+            if turn == 2 * CHUNKS - 1:
+                take_product()
             waiting.append((chunk, upper))
-            for row_tile in going_back[1:]:
-                if turn < 2 * CHUNKS - 3:
-                    transpose_back(row_tile, "step_n", 2)
-                else:
-                    transpose_back(row_tile, "words_t", 2)
+            for row_tile in going_back[len(first) :]:
+                transpose_back(row_tile, "step_n", 2)
                 finish(row_tile)
         take_product()
         for row_tile in rows:

@@ -275,7 +275,7 @@ def tile_liquidcell_pa_t_kernel(
 
         def vector_rates(chunk):
             if chunk < EARLY:
-                return (0, 2)
+                return (0, 1, 2)
             if chunk < CHUNKS - 1:
                 return (0,)
             return ()
@@ -386,6 +386,13 @@ def tile_liquidcell_pa_t_kernel(
                     rows.extend([(half[0], t) for t in range(SIZES[half[0]])])
             waiting.clear()
 
+        def take_rates(units):
+            for unit in units:
+                if unit[1] in vector_rates(unit[0]):
+                    rate_on_vector(unit)
+                else:
+                    rate_on_scalar(unit)
+
         for turn in range(2 * CHUNKS):
             chunk, upper = divmod(turn, 2)
             units = [(chunk, 2 * upper), (chunk, 2 * upper + 1)]
@@ -402,6 +409,9 @@ def tile_liquidcell_pa_t_kernel(
                 take_product()
             if ahead and chunk > 0:
                 quantize(chunk + 1, upper)
+            last = turn == 2 * CHUNKS - 1
+            if last:
+                take_rates(units)
             first = going_back if turn >= 2 * CHUNKS - 4 else going_back[:1]
             for row_tile in first:
                 if turn < 2 * CHUNKS - 3 or row_tile is first[0]:
@@ -409,13 +419,10 @@ def tile_liquidcell_pa_t_kernel(
                 else:
                     transpose_back(row_tile, "words_t", 2)
                 finish(row_tile)
-            for unit in units:
-                if unit[1] in vector_rates(chunk):
-                    rate_on_vector(unit)
-                else:
-                    rate_on_scalar(unit)
+            if not last:
+                take_rates(units)
             meet_hidden((chunk, upper))
-            if turn == 2 * CHUNKS - 1:
+            if last:
                 take_product()
             waiting.append((chunk, upper))
             for row_tile in going_back[len(first) :]:

@@ -276,8 +276,8 @@ def tile_liquidcell_pa_t_kernel(
         def vector_rates(chunk):
             if chunk < EARLY:
                 return (0, 1, 2)
-            if chunk < CHUNKS - 1:
-                return (0,)
+            if chunk < CHUNKS - 2:
+                return (2,)
             return ()
 
         def rate_on_scalar(unit):

import math
from contextlib import ExitStack

import concourse.mybir as mybir
from concourse.masks import make_identity

F32 = mybir.dt.float32
BF16 = mybir.dt.bfloat16
U8 = mybir.dt.uint8
U32 = mybir.dt.uint32
I32 = mybir.dt.int32
FP8X4 = mybir.dt.float8_e4m3fn_x4
TANH = mybir.ActivationFunctionType.Tanh
IDENTITY = mybir.ActivationFunctionType.Identity
ALU = mybir.AluOpType

P = 128
PACK = 4
BATCH = 4096
FEATURES = 512
WORDS = FEATURES // 2
ROW_TILES = BATCH // P
SIZES = (2, 4, 4, 4, 4, 4, 4, 4, 2)
STARTS = tuple(sum(SIZES[:c]) for c in range(len(SIZES)))
CHUNKS = len(SIZES)
WIDEST = max(SIZES) * P
FEATURE_TILES = FEATURES // P

SPLIT = (CHUNKS - 2,)

W_TAU_X = 0
W_TAU_H = 1
W_IN = 2
W_REC = 3

EARLY = 3

FLOPS = 4 * 2 * BATCH * FEATURES * FEATURES


def tile_liquidcell_pa_t_kernel(
    tc,
    x,
    hidden,
    W_rec_words,
    W_rec_scales,
    W_in_w_words,
    W_in_w_scales,
    W_in_b,
    tau_base,
    tau_adapt_w_words,
    tau_adapt_w_scales,
    tau_adapt_b,
    out,
):
    nc = tc.nc

    x_rows = x.rearrange("(p i) k -> p i k", i=ROW_TILES)
    h_rows = hidden.rearrange("(p i) k -> p i k", i=ROW_TILES)
    out_rows = out.rearrange("(p i) f -> p i f", i=ROW_TILES)

    with ExitStack() as stack:
        consts = stack.enter_context(tc.tile_pool(name="consts", bufs=1))
        stage = stack.enter_context(tc.tile_pool(name="stage", bufs=3))
        work = stack.enter_context(tc.tile_pool(name="work", bufs=3))
        psum = stack.enter_context(tc.psum_pool(name="psum", bufs=1))
        stack.enter_context(tc.manual_schedule())

        x_nat = [consts.tile([P, SIZES[c], FEATURES], BF16, name="x_nat%d" % c) for c in range(CHUNKS)]
        h_nat = [consts.tile([P, SIZES[c], FEATURES], BF16, name="h_nat%d" % c) for c in range(CHUNKS)]

        def load(natural, rows, c, queue):
            queue.dma_start(out=natural[c][:], in_=rows[:, STARTS[c] : STARTS[c] + SIZES[c], :])

        load(x_nat, x_rows, 0, nc.sync)
        load(h_nat, h_rows, 0, nc.sync)

        tau_scales_raw = consts.tile([P, 2, FEATURES], U8, align_bytes=64)
        nc.vector.memset(tau_scales_raw[:].rearrange("p w n -> p (w n)").bitcast(I32), 0)
        cell_scales_raw = consts.tile([P, 2, FEATURES], U8, align_bytes=64)
        nc.vector.memset(cell_scales_raw[:].rearrange("p w n -> p (w n)").bitcast(I32), 0)
        quads = [(slice(4 * q, 4 * q + 4), slice(32 * q, 32 * q + 4)) for q in range(4)]
        for rows, parts in quads:
            nc.sync.dma_start(
                out=tau_scales_raw[parts, :, :].bitcast(I32),
                in_=tau_adapt_w_scales[:, rows, :].rearrange("g r n -> r g n").bitcast(I32),
            )

        raw_codes = consts.tile([P, 4, FEATURES], I32, align_bytes=64)
        nc.sync.dma_start(
            out=raw_codes[:, W_TAU_X : W_TAU_H + 1, :],
            in_=tau_adapt_w_words.rearrange("g p n t -> p g (n t)").bitcast(I32),
        )
        def load_vector(vec, name):
            vector = consts.tile([P, FEATURE_TILES], BF16, name=name)
            nc.sync.dma_start(out=vector[:], in_=vec.rearrange("(p j) -> p j", j=FEATURE_TILES))
            return vector

        gate_vector = load_vector(tau_adapt_b, "gate_vector")
        nc.sync.dma_start(out=raw_codes[:, W_IN, :], in_=W_in_w_words[0].rearrange("p n t -> p (n t)").bitcast(I32))
        nc.sync.dma_start(out=raw_codes[:, W_REC, :], in_=W_rec_words[0].rearrange("p n t -> p (n t)").bitcast(I32))
        for rows, parts in quads:
            lower = slice(parts.start + 4, parts.stop + 4)
            nc.sync.dma_start(out=cell_scales_raw[lower, 0, :].bitcast(I32), in_=W_in_w_scales[0, rows, :].bitcast(I32))
            nc.sync.dma_start(out=cell_scales_raw[lower, 1, :].bitcast(I32), in_=W_rec_scales[0, rows, :].bitcast(I32))
        in_vector = load_vector(W_in_b, "in_vector")
        tau_vector = load_vector(tau_base, "tau_vector")
        for c in range(2, CHUNKS):
            load(x_nat, x_rows, c, nc.sync)
            load(h_nat, h_rows, c, nc.sync)

        ident_f32 = consts.tile([P, P], F32)
        make_identity(nc, ident_f32[:])

        load(x_nat, x_rows, 1, nc.gpsimd)
        load(h_nat, h_rows, 1, nc.gpsimd)

        zeros = consts.tile([P, 4 * P], BF16)
        nc.vector.memset(zeros[:], 0.0)

        def keep_warm(count):
            for repeat in range(count):
                unread = psum.tile([P, 4 * P], F32, tag="step_n", bufs=2)
                nc.tensor.matmul(unread[:], lhsT=zeros[:, 0:P], rhs=zeros[:], start=True, stop=True)

        zero_col = consts.tile([P, 1], F32)
        nc.vector.memset(zero_col[:], 0.0)
        warm_col = consts.tile([P, 1], F32)
        nc.scalar.activation(out=warm_col[:], in_=zero_col[:], func=TANH)

        tau_scales = consts.tile([P, 2, FEATURES], U8, align_bytes=64)
        cell_scales = consts.tile([P, 2, FEATURES], U8, align_bytes=64)
        w_codes = consts.tile([P, 4, FEATURES], I32, align_bytes=64)

        def arrange(out, in_, half):
            tiles = slice(2 * half, 2 * half + 2)
            nc.vector.tensor_copy(
                out=out.rearrange("p w (j m) -> p w j m", j=FEATURE_TILES)[:, :, tiles, :],
                in_=in_.rearrange("p w (m j) -> p w j m", j=FEATURE_TILES)[:, :, tiles, :],
            )

        def arrange_gate(half):
            arrange(tau_scales[:], tau_scales_raw[:], half)
            arrange(w_codes[:, W_TAU_X:W_IN, :], raw_codes[:, W_TAU_X:W_IN, :], half)

        def arrange_cell(half):
            arrange(cell_scales[:], cell_scales_raw[:], half)
            arrange(w_codes[:, W_IN : W_REC + 1, :], raw_codes[:, W_IN : W_REC + 1, :], half)

        neg_in_bias = consts.tile([P, FEATURE_TILES], F32)
        gate_bias = consts.tile([P, FEATURE_TILES], F32)
        inv_tau = consts.tile([P, FEATURE_TILES], F32)
        rate = consts.tile([P, FEATURE_TILES], F32)
        neg_two_rate = consts.tile([P, FEATURE_TILES], F32)

        def prepare_gate_bias():
            nc.vector.tensor_scalar(
                out=gate_bias[:],
                in0=gate_vector[:],
                scalar1=0.5,
                scalar2=0.5 * math.log(3.0),
                op0=ALU.mult,
                op1=ALU.add,
            )

        def prepare_in_bias():
            nc.vector.tensor_scalar_mul(out=neg_in_bias[:], in0=in_vector[:], scalar1=-1.0)

        def prepare_rates():
            nc.vector.reciprocal(out=inv_tau[:], in_=tau_vector[:])
            nc.vector.tensor_scalar_mul(out=rate[:], in0=inv_tau[:], scalar1=0.2 / 3.0)
            nc.vector.tensor_scalar_mul(out=neg_two_rate[:], in0=inv_tau[:], scalar1=-0.4 / 3.0)

        grouped = {}
        act = {}

        def transpose_in(chunk, operand):
            natural = (x_nat, h_nat)[operand][chunk]
            grouped[(chunk, operand)] = stage.tile(
                [P, PACK * WIDEST], BF16, name="grouped%d" % operand, bufs=3 + operand, align_bytes=64
            )
            packed = grouped[(chunk, operand)][:].bitcast(F32)
            for pair in range(SIZES[chunk] // 2):
                words_t = psum.tile([P, 2, 2, P], F32, name="words_t", bufs=2)
                for t in range(2):
                    words = natural[:, 2 * pair + t, :].bitcast(F32)
                    for u in range(2):
                        nc.tensor.transpose(words_t[:, t, u, :], words[:, u:WORDS:2], ident_f32[:])
                half = slice(pair * 4 * P, (pair + 1) * 4 * P)
                nc.scalar.copy(
                    out=packed[:, half].rearrange("p (t r u) -> p t r u", t=2, u=2),
                    in_=words_t[:].rearrange("p t u r -> p t r u"),
                )

        def quantize(chunk, operand):
            width = SIZES[chunk] * P
            codes = stage.tile([P, WIDEST], U32, name="codes%d" % operand, align_bytes=64)
            scales = stage.tile([P, WIDEST], U8, name="scales%d" % operand, align_bytes=64)
            nc.vector.quantize_mx(
                out=codes[:, 0:width].bitcast(FP8X4),
                scales=scales[:, 0:width],
                in_=grouped[(chunk, operand)][:, 0 : PACK * width],
            )
            act[(chunk, operand)] = (codes, scales)

        gates = {}
        cells = {}
        step_t = {}
        kept_t = {}

        def mx_pass(acc, weight, cols, chunk, operand, first):
            width = SIZES[chunk] * P
            codes, scales = act[(chunk, operand)]
            if weight < W_IN:
                w_scale = tau_scales[:, weight, cols]
            else:
                w_scale = cell_scales[4:P, weight - W_IN, cols]
            nc.tensor.matmul_mx(
                out=acc[:, 0:width],
                lhsT=w_codes[:, weight, cols].bitcast(FP8X4),
                lhsT_scale=w_scale,
                rhs=codes[:, 0:width].bitcast(FP8X4),
                rhs_scale=scales[:, 0:width],
                start=first,
                stop=not first,
            )

        def gate_in(unit):
            chunk, j = unit
            width = SIZES[chunk] * P
            cols = slice(j * P, (j + 1) * P)
            half = (chunk, j // 2)
            if j % 2 == 0:
                gates[half] = work.tile([P, 2, WIDEST], F32, name="gate", bufs=4)
            gate_sum = psum.tile([P, WIDEST], F32, tag="sums", bufs=4)
            mx_pass(gate_sum, W_TAU_X, cols, chunk, 0, True)
            mx_pass(gate_sum, W_TAU_H, cols, chunk, 1, False)
            nc.scalar.activation(
                out=gates[half][:, j % 2, 0:width],
                in_=gate_sum[:, 0:width],
                func=TANH,
                bias=gate_bias[:, j : j + 1],
                scale=0.5,
            )

        def cell_in(unit):
            chunk, j = unit
            width = SIZES[chunk] * P
            cols = slice(j * P, (j + 1) * P)
            half = (chunk, j // 2)
            if j % 2 == 0:
                cells[half] = work.tile([P, 2, WIDEST], F32, name="cell", bufs=4)
            cell_sum = psum.tile([P, WIDEST], F32, tag="sums", bufs=4)
            mx_pass(cell_sum, W_IN, cols, chunk, 0, True)
            mx_pass(cell_sum, W_REC, cols, chunk, 1, False)
            nc.scalar.activation(
                out=cells[half][:, j % 2, 0:width],
                in_=cell_sum[:, 0:width],
                func=TANH,
                bias=neg_in_bias[:, j : j + 1],
                scale=-1.0,
            )

        def rate_on_vector(unit):
            chunk, j = unit
            gate = gates[(chunk, j // 2)][:, j % 2, 0 : SIZES[chunk] * P]
            nc.vector.tensor_scalar(
                out=gate,
                in0=gate,
                scalar1=rate[:, j : j + 1],
                scalar2=neg_two_rate[:, j : j + 1],
                op0=ALU.mult,
                op1=ALU.add,
            )

        def vector_rates(chunk):
            if chunk < EARLY:
                return (0, 1, 2)
            if chunk < CHUNKS - 2:
                return (2,)
            return ()

        def rate_on_scalar(unit):
            chunk, j = unit
            gate = gates[(chunk, j // 2)][:, j % 2, 0 : SIZES[chunk] * P]
            nc.scalar.activation(
                out=gate, in_=gate, func=IDENTITY, bias=neg_two_rate[:, j : j + 1], scale=rate[:, j : j + 1]
            )

        def meet_hidden(half):
            chunk, upper = half
            width = SIZES[chunk] * P
            tiles = slice(2 * upper, 2 * upper + 2)
            h_t = grouped[(chunk, 1)][:, 0 : PACK * width].rearrange("p (n j) -> p j n", j=PACK)[:, tiles, :]
            cell = cells[half][:, :, 0:width]
            if chunk in SPLIT:
                if upper == 0:
                    kept_t[chunk] = work.tile([P, FEATURE_TILES, WIDEST], F32, name="kept_t", bufs=1)
                nc.vector.scalar_tensor_tensor(
                    out=kept_t[chunk][:, tiles, 0:width],
                    in0=gates[half][:, :, 0:width],
                    scalar=1.0,
                    in1=h_t,
                    op0=ALU.add,
                    op1=ALU.mult,
                )
            else:
                nc.vector.tensor_tensor(out=cell, in0=cell, in1=h_t, op=ALU.add)

        def multiply_out(half):
            chunk, upper = half
            width = SIZES[chunk] * P
            tiles = slice(2 * upper, 2 * upper + 2)
            if upper == 0:
                step_t[chunk] = work.tile([P, FEATURE_TILES, WIDEST], F32, name="step_t")
            nc.vector.tensor_tensor(
                out=step_t[chunk][:, tiles, 0:width],
                in0=gates[half][:, :, 0:width],
                in1=cells[half][:, :, 0:width],
                op=ALU.mult,
            )

        back = {}

        def transpose_back(row_tile, tag, bufs):
            chunk, t = row_tile
            rows = slice(t * P, (t + 1) * P)
            step_n = psum.tile([P, FEATURE_TILES, P], F32, tag=tag, bufs=bufs)
            for j in range(FEATURE_TILES):
                if chunk in SPLIT:
                    parts = (step_t[chunk], kept_t[chunk])
                else:
                    parts = (step_t[chunk],)
                for part in parts:
                    nc.tensor.matmul(
                        step_n[:, j, :],
                        lhsT=part[:, j, rows],
                        rhs=ident_f32[:],
                        is_transpose=True,
                        start=part is parts[0],
                        stop=part is parts[-1],
                    )
            back[row_tile] = step_n

        def finish(row_tile):
            chunk, t = row_tile
            result = work.tile([P, FEATURES], F32, bufs=8)
            out_view = result[:].rearrange("p (m j) -> p m j", j=FEATURE_TILES)
            step_view = back[row_tile][:].rearrange("p j m -> p m j")
            if chunk in SPLIT:
                nc.scalar.copy(out=out_view, in_=step_view)
            else:
                nc.vector.tensor_tensor(
                    out=out_view,
                    in0=step_view,
                    in1=h_nat[chunk][:, t, :].rearrange("p (m j) -> p m j", j=FEATURE_TILES),
                    op=ALU.add,
                )
            nc.sync.dma_start(out=out_rows[:, STARTS[chunk] + t, :], in_=result[:])

        keep_warm(2)
        transpose_in(0, 0)
        transpose_in(0, 1)
        keep_warm(4)
        arrange_gate(0)
        quantize(0, 0)
        quantize(0, 1)
        prepare_gate_bias()
        arrange_gate(1)
        for upper in range(2):
            for j in range(2 * upper, 2 * upper + 2):
                gate_in((0, j))
            transpose_in(1, upper)
        arrange_cell(0)
        arrange_cell(1)
        prepare_in_bias()
        prepare_rates()
        quantize(1, 0)
        quantize(1, 1)
        waiting = []
        rows = []
        def take_product():
            for half in waiting:
                multiply_out(half)
                if half[1] == 1:
                    rows.extend([(half[0], t) for t in range(SIZES[half[0]])])
            waiting.clear()

        def take_rates(units):
            for unit in units:
                if unit[1] in vector_rates(unit[0]):
                    rate_on_vector(unit)
                else:
                    rate_on_scalar(unit)

        for turn in range(2 * CHUNKS):
            chunk, upper = divmod(turn, 2)
            units = [(chunk, 2 * upper), (chunk, 2 * upper + 1)]
            going_back = rows[:2]
            rows[:] = rows[2:]
            ahead = chunk + 1 < CHUNKS
            if ahead and chunk > 0:
                transpose_in(chunk + 1, upper)
            for unit in units:
                if chunk > 0:
                    gate_in(unit)
                cell_in(unit)
            if turn < 2 * CHUNKS - 1:
                take_product()
            if ahead and chunk > 0:
                quantize(chunk + 1, upper)
            last = turn == 2 * CHUNKS - 1
            if last:
                take_rates(units)
            first = going_back if turn >= 2 * CHUNKS - 4 else going_back[:1]
            for row_tile in first:
                if turn < 2 * CHUNKS - 3 or row_tile is first[0]:
                    transpose_back(row_tile, "step_n", 2)
                else:
                    transpose_back(row_tile, "words_t", 2)
                finish(row_tile)
            if not last:
                take_rates(units)
            meet_hidden((chunk, upper))
            if last:
                take_product()
            waiting.append((chunk, upper))
            for row_tile in going_back[len(first) :]:
                transpose_back(row_tile, "step_n", 2)
                finish(row_tile)
        take_product()
        for row_tile in rows:
            transpose_back(row_tile, "sums", 4)
            finish(row_tile)
